import numpy as np
import ml_dtypes


def mxq(x, axis, fmt="e4m3"):
    dtype, down = {"e4m3": (ml_dtypes.float8_e4m3fn, 7), "e5m2": (ml_dtypes.float8_e5m2, 14)}[fmt]
    v = np.moveaxis(np.asarray(x, np.float32).astype(ml_dtypes.bfloat16).astype(np.float64), axis, -1)
    blocks = v.reshape(v.shape[:-1] + (-1, 32))
    amax = np.abs(blocks).max(-1, keepdims=True)
    byte = np.maximum(np.where(amax > 0, np.frexp(amax)[1] - 1 + 127, 0) - down, 1)
    scale = np.exp2(byte - 127.0)
    codes = (blocks / scale).astype(np.float32).astype(dtype).astype(np.float64)
    return np.moveaxis((codes * scale).reshape(v.shape), -1, axis)


WIDE = False


def mx_kscale(k):
    if not WIDE:
        return np.ones(k)
    levels = np.array([10, -10, 5, -5, 0])
    if k % 512:
        return np.exp2(np.random.permutation(np.resize(levels, k // 32))).repeat(32)
    a = np.empty((k // 512, 16))
    for p in range(k // 512):
        a[p, :8] = np.random.permutation(np.resize(levels, 8))
        for g in range(8):
            far = levels[np.abs(levels - a[p, g]) >= 10]
            a[p, g + 8] = far[np.random.randint(len(far))]
    return np.exp2(a.ravel()).repeat(32)


BF16 = ml_dtypes.bfloat16


def bf(x):
    return np.asarray(x, np.float32).astype(BF16)


def f64(x):
    return np.asarray(x).astype(np.float64)


N, E, HD, H1, H3, DM = 16384, 512, 256, 1024, 128, 1024
C = 2 * HD


def setup_inputs():
    s = mx_kscale(N)
    t = mx_kscale(C)
    r = np.concatenate([np.full(HD, 2.0 / np.sqrt(HD)), np.full(HD, 8.0 / np.sqrt(N * HD))])
    return {
        "H_A": bf(np.random.standard_normal((N, E)) * 0.25 * s[:, None]),
        "H_mean_A": bf(np.random.standard_normal((N, HD)) * 0.35 / s[:, None] * t[HD:]),
        "H_mean_M": bf(np.random.standard_normal((E, HD)) * 0.35 * t[:HD]),
        "wEA1": bf(np.random.standard_normal((C, H3)) * (r / t)[:, None]),
        "bEA1": bf(np.random.standard_normal(H3) * 0.1),
    }


def reference(H_A, H_mean_A, H_mean_M, wEA1, bEA1):
    sum_A = mxq(f64(H_A), 0, "e4m3").T @ mxq(f64(H_mean_A), 0, "e4m3")
    EventA = np.concatenate([f64(H_mean_M), sum_A], axis=1)
    return np.maximum((mxq(EventA, 1, "e4m3") @ mxq(f64(wEA1), 0, "e4m3")) + f64(bEA1), 0.0)

@@ -1,0 +1,186 @@
+from contextlib import ExitStack
+
+import concourse.mybir as mybir
+from concourse.masks import make_identity
+
+BF16 = mybir.dt.bfloat16
+F32 = mybir.dt.float32
+U32 = mybir.dt.uint32
+U8 = mybir.dt.uint8
+FP8X4 = mybir.dt.float8_e4m3fn_x4
+ADD = mybir.AluOpType.add
+
+P = 128
+PACK = 4
+K_PASS = P * PACK
+
+NODES, EVENTS, HD, H3 = 16384, 512, 256, 128
+FUSED = 2 * HD
+EVENT_TILES = EVENTS // P
+PAIR_TILES = 2
+PASSES = NODES // K_PASS
+
+ROUND_PASSES = 2
+ROUNDS = PASSES // ROUND_PASSES
+
+SCALAR_COLS = 320
+
+RUN = 4
+
+RAW_ROUNDS = 8
+WORK_ROUNDS = 3
+
+FLOPS = 2 * NODES * EVENTS * HD + 2 * EVENTS * FUSED * H3
+
+
+def regroup(copy, grouped, rows):
+    copy(
+        out=grouped.rearrange("p (c i) j -> p c j i", i=RUN),
+        in_=rows.rearrange("p j (c i) -> p c j i", i=RUN),
+    )
+
+
+def regroup_passes(copy, grouped, rows):
+    copy(
+        out=grouped.rearrange("p n (c i) j -> p n c j i", i=RUN),
+        in_=rows.rearrange("p n j (c i) -> p n c j i", i=RUN),
+    )
+
+
+def tile_mymodel_icdm_pa_k_kernel(tc, H_A, H_mean_A, H_mean_M, wEA1, bEA1, out):
+    nc = tc.nc
+    with ExitStack() as stack:
+        consts = stack.enter_context(tc.tile_pool(name="consts", bufs=1))
+        raw_pass = stack.enter_context(tc.tile_pool(name="raw_pass", bufs=RAW_ROUNDS * ROUND_PASSES))
+        raw_round = stack.enter_context(tc.tile_pool(name="raw_round", bufs=RAW_ROUNDS))
+        work_pass = stack.enter_context(tc.tile_pool(name="work_pass", bufs=WORK_ROUNDS * ROUND_PASSES))
+        work_round = stack.enter_context(tc.tile_pool(name="work_round", bufs=WORK_ROUNDS))
+        psum = stack.enter_context(tc.psum_pool(name="psum", bufs=1))
+        stack.enter_context(tc.manual_schedule())
+
+        def quantise(pool, name, grouped):
+            words = grouped.shape[1] // PACK
+            codes = pool.tile([P, words], U32, name=name + "_codes", tag=name + "_codes", align_bytes=64)
+            scales = pool.tile([P, words], U8, name=name + "_scales", tag=name + "_scales", align_bytes=64)
+            nc.vector.quantize_mx(out=codes[:].bitcast(FP8X4), scales=scales[:], in_=grouped)
+            return codes, scales
+
+        identity = consts.tile([P, P], F32)
+        make_identity(nc, identity[:])
+        ones = consts.tile([P, P], BF16)
+        nc.vector.memset(ones[:], 1.0)
+        bias_rows = consts.tile([P, H3], BF16)
+        nc.vector.memset(bias_rows[:], 0.0)
+
+        sums = [psum.tile([P, 2 * HD], F32, name="sum%d" % a) for a in range(EVENT_TILES)]
+
+        def load_events(t):
+            ha_rows = raw_pass.tile([P, PACK, EVENTS], BF16)
+            nc.sync.dma_start(
+                out=ha_rows[:].rearrange("p j e -> p (j e)"),
+                in_=H_A[t * K_PASS : (t + 1) * K_PASS, :].rearrange("(p j) e -> p (j e)", j=PACK),
+            )
+            return ha_rows
+
+        def load_features(t):
+            hm_rows = raw_round.tile([P, ROUND_PASSES, PACK, HD], BF16)
+            nc.sync.dma_start(
+                out=hm_rows[:].rearrange("p n j d -> p n (j d)"),
+                in_=H_mean_A[t * K_PASS : (t + ROUND_PASSES) * K_PASS, :].rearrange(
+                    "(n p j) d -> p n (j d)", p=P, j=PACK
+                ),
+            )
+            return hm_rows
+
+        def multiply(t, ha_codes, ha_scales, hm_codes, hm_scales):
+            first = (t % ROUND_PASSES) * HD
+            features = slice(first, first + HD)
+            for a in range(EVENT_TILES):
+                events = slice(a * P, (a + 1) * P)
+                nc.tensor.matmul_mx(
+                    out=sums[a][:, 0:HD],
+                    lhsT=ha_codes[:, events].bitcast(FP8X4),
+                    lhsT_scale=ha_scales[:, events],
+                    rhs=hm_codes[:, features].bitcast(FP8X4),
+                    rhs_scale=hm_scales[:, features],
+                    start=(t == 0),
+                    stop=(t == PASSES - 1),
+                )
+
+        for r in range(ROUNDS):
+            t = r * ROUND_PASSES
+            ha_rows_a = load_events(t)
+            hm_rows = load_features(t)
+            ha_rows_b = load_events(t + 1)
+
+            ha_grouped_a = work_pass.tile([P, EVENTS, PACK], BF16, tag="ha_grouped", align_bytes=64)
+            regroup(nc.scalar.copy, ha_grouped_a[:], ha_rows_a[:])
+            ha_grouped_b = work_pass.tile([P, EVENTS, PACK], BF16, tag="ha_grouped", align_bytes=64)
+            regroup(nc.scalar.copy, ha_grouped_b[:, 0:SCALAR_COLS, :], ha_rows_b[:, :, 0:SCALAR_COLS])
+
+            hm_grouped = work_round.tile([P, ROUND_PASSES, HD, PACK], BF16, align_bytes=64)
+            regroup_passes(nc.vector.tensor_copy, hm_grouped[:], hm_rows[:])
+            ha_a = quantise(work_pass, "ha", ha_grouped_a[:].rearrange("p e j -> p (e j)"))
+            regroup(nc.vector.tensor_copy, ha_grouped_b[:, SCALAR_COLS:EVENTS, :], ha_rows_b[:, :, SCALAR_COLS:EVENTS])
+            hm = quantise(work_round, "hm", hm_grouped[:].rearrange("p n d j -> p (n d j)"))
+            multiply(t, ha_a[0], ha_a[1], hm[0], hm[1])
+
+            if r == ROUNDS - 1:
+                event_rows = consts.tile([P, EVENT_TILES, FUSED], BF16)
+                nc.sync.dma_start(out=event_rows[:, :, 0:HD], in_=H_mean_M.rearrange("(a p) c -> p a c", p=P))
+                w_rows = consts.tile([P, PACK, H3], BF16)
+                nc.sync.dma_start(out=w_rows[:], in_=wEA1.rearrange("(p j) h -> p j h", j=PACK))
+                nc.sync.dma_start(out=bias_rows[0:1, :], in_=bEA1.rearrange("(o h) -> o h", o=1))
+
+            ha_b = quantise(work_pass, "ha", ha_grouped_b[:].rearrange("p e j -> p (e j)"))
+            multiply(t + 1, ha_b[0], ha_b[1], hm[0], hm[1])
+
+        for a in range(EVENT_TILES):
+            copy = nc.vector.tensor_copy if a % 2 == 0 else nc.scalar.copy
+            copy(out=event_rows[:, a, HD:FUSED], in_=sums[a][:, 0:HD])
+        words = event_rows[:].rearrange("p a c -> p (a c)").bitcast(F32)
+        event_words = FUSED // 2
+        word_t = [psum.tile([P, PAIR_TILES, 2, P], F32, name="word_t%d" % b) for b in range(EVENT_TILES // PAIR_TILES)]
+        for a in range(EVENT_TILES):
+            for u in range(2):
+                nc.tensor.transpose(
+                    word_t[a // PAIR_TILES][:, a % PAIR_TILES, u, :],
+                    words[:, a * event_words + u : (a + 1) * event_words : 2],
+                    identity[:],
+                )
+        fused_grouped = consts.tile([P, EVENTS, PACK], BF16, align_bytes=64)
+        fused_words = fused_grouped[:].rearrange("p e j -> p (e j)").bitcast(F32)
+        for b in range(EVENT_TILES // PAIR_TILES):
+            copy = nc.vector.tensor_copy if b % 2 == 0 else nc.scalar.copy
+            size = PAIR_TILES * P * 2
+            copy(
+                out=fused_words[:, b * size : (b + 1) * size].rearrange("p (a r u) -> p a r u", a=PAIR_TILES, u=2),
+                in_=word_t[b][:].rearrange("p a u r -> p a r u"),
+            )
+        w_grouped = consts.tile([P, H3, PACK], BF16, align_bytes=64)
+        regroup(nc.scalar.copy, w_grouped[:], w_rows[:])
+        w = quantise(consts, "w", w_grouped[:].rearrange("p h j -> p (h j)"))
+        fused = quantise(consts, "fused", fused_grouped[:].rearrange("p e j -> p (e j)"))
+
+        bias_ps = psum.tile([P, H3], F32)
+        nc.tensor.matmul(out=bias_ps[:], lhsT=ones[:], rhs=bias_rows[:], start=True, stop=True)
+        bias_all = consts.tile([P, H3], F32)
+        nc.vector.tensor_copy(out=bias_all[:], in_=bias_ps[:])
+
+        out_ps = psum.tile([P, EVENT_TILES, H3], F32)
+        for a in range(EVENT_TILES):
+            nc.tensor.matmul_mx(
+                out=out_ps[:, a, :],
+                lhsT=fused[0][:, a * P : (a + 1) * P].bitcast(FP8X4),
+                lhsT_scale=fused[1][:, a * P : (a + 1) * P],
+                rhs=w[0][:].bitcast(FP8X4),
+                rhs_scale=w[1][:],
+                start=True,
+                stop=True,
+            )
+        result = consts.tile([P, EVENT_TILES, H3], F32)
+        nc.vector.tensor_tensor(
+            out=result[:], in0=out_ps[:], in1=bias_all[:].unsqueeze(1).to_broadcast([P, EVENT_TILES, H3]), op=ADD
+        )
+        nc.vector.tensor_scalar_max(out=result[:], in0=result[:], scalar1=0.0)
+        nc.sync.dma_start(out=out.rearrange("(a p) h -> p a h", p=P), in_=result[:])

@@ -9,6 +9,7 @@ U32 = mybir.dt.uint32
 U8 = mybir.dt.uint8
 FP8X4 = mybir.dt.float8_e4m3fn_x4
 ADD = mybir.AluOpType.add
+RELU = mybir.ActivationFunctionType.Relu
 
 P = 128
 PACK = 4
@@ -17,7 +18,6 @@ K_PASS = P * PACK
 NODES, EVENTS, HD, H3 = 16384, 512, 256, 128
 FUSED = 2 * HD
 EVENT_TILES = EVENTS // P
-PAIR_TILES = 2
 PASSES = NODES // K_PASS
 
 ROUND_PASSES = 2
@@ -26,6 +26,8 @@ ROUNDS = PASSES // ROUND_PASSES
 SCALAR_COLS = 320
 
 RUN = 4
+
+SMALL_LOAD_ROUND = 4
 
 RAW_ROUNDS = 8
 WORK_ROUNDS = 3
@@ -56,6 +58,7 @@ def tile_mymodel_icdm_pa_k_kernel(tc, H_A, H_mean_A, H_mean_M, wEA1, bEA1, out):
         work_pass = stack.enter_context(tc.tile_pool(name="work_pass", bufs=WORK_ROUNDS * ROUND_PASSES))
         work_round = stack.enter_context(tc.tile_pool(name="work_round", bufs=WORK_ROUNDS))
         psum = stack.enter_context(tc.psum_pool(name="psum", bufs=1))
+        psum_ring = stack.enter_context(tc.psum_pool(name="psum_ring", bufs=2))
         stack.enter_context(tc.manual_schedule())
 
         def quantise(pool, name, grouped):
@@ -104,14 +107,34 @@ def tile_mymodel_icdm_pa_k_kernel(tc, H_A, H_mean_A, H_mean_M, wEA1, bEA1, out):
                     rhs=hm_codes[:, features].bitcast(FP8X4),
                     rhs_scale=hm_scales[:, features],
                     start=(t == 0),
-                    stop=(t == PASSES - 1),
+                    stop=False,
                 )
 
-        for r in range(ROUNDS):
+        def load_small():
+            event_rows = consts.tile([P, EVENT_TILES, FUSED], BF16)
+            nc.sync.dma_start(out=event_rows[:, :, 0:HD], in_=H_mean_M.rearrange("(a p) c -> p a c", p=P))
+            w_rows = consts.tile([P, PACK, H3], BF16)
+            nc.sync.dma_start(out=w_rows[:], in_=wEA1.rearrange("(p j) h -> p j h", j=PACK))
+            nc.sync.dma_start(out=bias_rows[0:1, :], in_=bEA1.rearrange("(o h) -> o h", o=1))
+            return event_rows, w_rows
+
+        def prepare_small(w_rows):
+            w_grouped = consts.tile([P, H3, PACK], BF16, align_bytes=64)
+            regroup(nc.scalar.copy, w_grouped[:], w_rows[:])
+            bias_ps = psum_ring.tile([P, 4 * H3], F32, tag="out_ps")
+            nc.tensor.matmul(out=bias_ps[:, 0:H3], lhsT=ones[:], rhs=bias_rows[:], start=True, stop=True)
+            bias_all = consts.tile([P, H3], F32)
+            nc.vector.tensor_copy(out=bias_all[:], in_=bias_ps[:, 0:H3])
+            w = quantise(consts, "w", w_grouped[:].rearrange("p h j -> p (h j)"))
+            return w, bias_all
+
+        for r in range(ROUNDS - 1):
             t = r * ROUND_PASSES
             ha_rows_a = load_events(t)
             hm_rows = load_features(t)
             ha_rows_b = load_events(t + 1)
+            if r == SMALL_LOAD_ROUND:
+                event_rows, w_rows = load_small()
 
             ha_grouped_a = work_pass.tile([P, EVENTS, PACK], BF16, tag="ha_grouped", align_bytes=64)
             regroup(nc.scalar.copy, ha_grouped_a[:], ha_rows_a[:])
@@ -124,63 +147,134 @@ def tile_mymodel_icdm_pa_k_kernel(tc, H_A, H_mean_A, H_mean_M, wEA1, bEA1, out):
             regroup(nc.vector.tensor_copy, ha_grouped_b[:, SCALAR_COLS:EVENTS, :], ha_rows_b[:, :, SCALAR_COLS:EVENTS])
             hm = quantise(work_round, "hm", hm_grouped[:].rearrange("p n d j -> p (n d j)"))
             multiply(t, ha_a[0], ha_a[1], hm[0], hm[1])
-
-            if r == ROUNDS - 1:
-                event_rows = consts.tile([P, EVENT_TILES, FUSED], BF16)
-                nc.sync.dma_start(out=event_rows[:, :, 0:HD], in_=H_mean_M.rearrange("(a p) c -> p a c", p=P))
-                w_rows = consts.tile([P, PACK, H3], BF16)
-                nc.sync.dma_start(out=w_rows[:], in_=wEA1.rearrange("(p j) h -> p j h", j=PACK))
-                nc.sync.dma_start(out=bias_rows[0:1, :], in_=bEA1.rearrange("(o h) -> o h", o=1))
-
             ha_b = quantise(work_pass, "ha", ha_grouped_b[:].rearrange("p e j -> p (e j)"))
             multiply(t + 1, ha_b[0], ha_b[1], hm[0], hm[1])
+            if r == SMALL_LOAD_ROUND + 1:
+                w, bias_all = prepare_small(w_rows)
 
-        for a in range(EVENT_TILES):
-            copy = nc.vector.tensor_copy if a % 2 == 0 else nc.scalar.copy
-            copy(out=event_rows[:, a, HD:FUSED], in_=sums[a][:, 0:HD])
+        t = (ROUNDS - 1) * ROUND_PASSES
+        hm_rows = load_features(t)
+        ha_rows = raw_pass.tile([P, ROUND_PASSES, PACK, EVENTS], BF16, name="ha_rows_last", tag="ha_rows_last", bufs=1)
+        for n in range(ROUND_PASSES):
+            nc.sync.dma_start(
+                out=ha_rows[:, n].rearrange("p j e -> p (j e)"),
+                in_=H_A[(t + n) * K_PASS : (t + n + 1) * K_PASS, :].rearrange("(p j) e -> p (j e)", j=PACK),
+            )
+        tile_grouped = consts.tile([P, EVENT_TILES, ROUND_PASSES, P, PACK], BF16, align_bytes=64)
+        fused_grouped = consts.tile([P, EVENT_TILES, P, PACK], BF16, align_bytes=64)
+        result = consts.tile([P, EVENT_TILES, H3], F32)
         words = event_rows[:].rearrange("p a c -> p (a c)").bitcast(F32)
         event_words = FUSED // 2
-        word_t = [psum.tile([P, PAIR_TILES, 2, P], F32, name="word_t%d" % b) for b in range(EVENT_TILES // PAIR_TILES)]
-        for a in range(EVENT_TILES):
+
+        def tile_copy(copy, a, first=0, last=P):
+            regroup_passes(
+                copy, tile_grouped[:, a, :, first:last, :], ha_rows[:, :, :, a * P + first : a * P + last]
+            )
+
+        def tile_quantise(a):
+            return quantise(work_round, "tile", tile_grouped[:, a].rearrange("p n e j -> p (n e j)"))
+
+        def tile_multiply(a, codes, scales):
+            for n in range(ROUND_PASSES):
+                nc.tensor.matmul_mx(
+                    out=sums[a][:, 0:HD],
+                    lhsT=codes[:, n * P : (n + 1) * P].bitcast(FP8X4),
+                    lhsT_scale=scales[:, n * P : (n + 1) * P],
+                    rhs=hm[0][:, n * HD : (n + 1) * HD].bitcast(FP8X4),
+                    rhs_scale=hm[1][:, n * HD : (n + 1) * HD],
+                    start=False,
+                    stop=(n == ROUND_PASSES - 1),
+                )
+
+        def tile_sum(copy, a):
+            copy(out=event_rows[:, a, HD:FUSED], in_=sums[a][:, 0:HD])
+
+        def tile_transpose(a):
+            word_t = psum_ring.tile([P, 4, P], F32, tag="word_t")
             for u in range(2):
                 nc.tensor.transpose(
-                    word_t[a // PAIR_TILES][:, a % PAIR_TILES, u, :],
-                    words[:, a * event_words + u : (a + 1) * event_words : 2],
-                    identity[:],
+                    word_t[:, u, :], words[:, a * event_words + u : (a + 1) * event_words : 2], identity[:]
                 )
-        fused_grouped = consts.tile([P, EVENTS, PACK], BF16, align_bytes=64)
-        fused_words = fused_grouped[:].rearrange("p e j -> p (e j)").bitcast(F32)
-        for b in range(EVENT_TILES // PAIR_TILES):
-            copy = nc.vector.tensor_copy if b % 2 == 0 else nc.scalar.copy
-            size = PAIR_TILES * P * 2
+            return word_t
+
+        def tile_interleave(copy, a, word_t):
             copy(
-                out=fused_words[:, b * size : (b + 1) * size].rearrange("p (a r u) -> p a r u", a=PAIR_TILES, u=2),
-                in_=word_t[b][:].rearrange("p a u r -> p a r u"),
+                out=fused_grouped[:, a].rearrange("p e j -> p (e j)").bitcast(F32).rearrange("p (e u) -> p e u", u=2),
+                in_=word_t[:, 0:2, :].rearrange("p u e -> p e u"),
             )
-        w_grouped = consts.tile([P, H3, PACK], BF16, align_bytes=64)
-        regroup(nc.scalar.copy, w_grouped[:], w_rows[:])
-        w = quantise(consts, "w", w_grouped[:].rearrange("p h j -> p (h j)"))
-        fused = quantise(consts, "fused", fused_grouped[:].rearrange("p e j -> p (e j)"))
 
-        bias_ps = psum.tile([P, H3], F32)
-        nc.tensor.matmul(out=bias_ps[:], lhsT=ones[:], rhs=bias_rows[:], start=True, stop=True)
-        bias_all = consts.tile([P, H3], F32)
-        nc.vector.tensor_copy(out=bias_all[:], in_=bias_ps[:])
+        def tile_fused(a):
+            return quantise(work_round, "fused", fused_grouped[:, a].rearrange("p e j -> p (e j)"))
 
-        out_ps = psum.tile([P, EVENT_TILES, H3], F32)
-        for a in range(EVENT_TILES):
+        def tile_out(codes, scales):
+            out_ps = psum_ring.tile([P, 4 * H3], F32, tag="out_ps")
             nc.tensor.matmul_mx(
-                out=out_ps[:, a, :],
-                lhsT=fused[0][:, a * P : (a + 1) * P].bitcast(FP8X4),
-                lhsT_scale=fused[1][:, a * P : (a + 1) * P],
+                out=out_ps[:, 0:H3],
+                lhsT=codes[:].bitcast(FP8X4),
+                lhsT_scale=scales[:],
                 rhs=w[0][:].bitcast(FP8X4),
                 rhs_scale=w[1][:],
                 start=True,
                 stop=True,
             )
-        result = consts.tile([P, EVENT_TILES, H3], F32)
-        nc.vector.tensor_tensor(
-            out=result[:], in0=out_ps[:], in1=bias_all[:].unsqueeze(1).to_broadcast([P, EVENT_TILES, H3]), op=ADD
-        )
-        nc.vector.tensor_scalar_max(out=result[:], in0=result[:], scalar1=0.0)
-        nc.sync.dma_start(out=out.rearrange("(a p) h -> p a h", p=P), in_=result[:])
+            return out_ps
+
+        def tile_bias(a, out_ps):
+            nc.vector.tensor_tensor(out=result[:, a, :], in0=out_ps[:, 0:H3], in1=bias_all[:], op=ADD)
+
+        def tile_relu(a):
+            nc.scalar.activation(out=result[:, a, :], in_=result[:, a, :], func=RELU)
+
+        def store(first, last):
+            nc.sync.dma_start(
+                out=out[first * P : last * P, :].rearrange("(a p) h -> p a h", p=P), in_=result[:, first:last, :]
+            )
+
+        v_copy = nc.vector.tensor_copy
+        s_copy = nc.scalar.copy
+        hm_grouped = work_round.tile([P, ROUND_PASSES, HD, PACK], BF16, align_bytes=64)
+        regroup_passes(v_copy, hm_grouped[:], hm_rows[:])
+        tile_copy(s_copy, 0)
+        tile_copy(v_copy, 2)
+        hm = quantise(work_round, "hm", hm_grouped[:].rearrange("p n d j -> p (n d j)"))
+        q0 = tile_quantise(0)
+        tile_multiply(0, *q0)
+        tile_copy(s_copy, 1)
+        q2 = tile_quantise(2)
+        tile_multiply(2, *q2)
+        tile_copy(v_copy, 3, P // 2, P)
+        tile_copy(s_copy, 3, 0, P // 2)
+        q1 = tile_quantise(1)
+        tile_multiply(1, *q1)
+        tile_sum(v_copy, 0)
+        wt0 = tile_transpose(0)
+        q3 = tile_quantise(3)
+        tile_multiply(3, *q3)
+        tile_sum(s_copy, 2)
+        wt2 = tile_transpose(2)
+        tile_sum(s_copy, 1)
+        tile_interleave(v_copy, 0, wt0)
+        wt1 = tile_transpose(1)
+        tile_interleave(s_copy, 2, wt2)
+        tile_sum(v_copy, 3)
+        wt3 = tile_transpose(3)
+        f0 = tile_fused(0)
+        o0 = tile_out(*f0)
+        tile_interleave(s_copy, 1, wt1)
+        f2 = tile_fused(2)
+        o2 = tile_out(*f2)
+        tile_bias(0, o0)
+        tile_relu(0)
+        tile_interleave(v_copy, 3, wt3)
+        f1 = tile_fused(1)
+        o1 = tile_out(*f1)
+        f3 = tile_fused(3)
+        o3 = tile_out(*f3)
+        tile_bias(2, o2)
+        tile_relu(2)
+        tile_bias(1, o1)
+        tile_relu(1)
+        store(0, 3)
+        tile_bias(3, o3)
+        tile_relu(3)
+        store(3, 4)

@@ -23,7 +23,7 @@ PASSES = NODES // K_PASS
 ROUND_PASSES = 2
 ROUNDS = PASSES // ROUND_PASSES
 
-SCALAR_COLS = 320
+SCALAR_COLS = 256
 
 RUN = 4
 

@@ -23,7 +23,7 @@ PASSES = NODES // K_PASS
 ROUND_PASSES = 2
 ROUNDS = PASSES // ROUND_PASSES
 
-SCALAR_COLS = 256
+SCALAR_COLS = 288
 
 RUN = 4
 
@@ -85,13 +85,12 @@ def tile_mymodel_icdm_pa_k_kernel(tc, H_A, H_mean_A, H_mean_M, wEA1, bEA1, out):
             )
             return ha_rows
 
-        def load_features(t):
+        def load_features(r):
             hm_rows = raw_round.tile([P, ROUND_PASSES, PACK, HD], BF16)
+            first = r * ROUND_PASSES * K_PASS
             nc.sync.dma_start(
                 out=hm_rows[:].rearrange("p n j d -> p n (j d)"),
-                in_=H_mean_A[t * K_PASS : (t + ROUND_PASSES) * K_PASS, :].rearrange(
-                    "(n p j) d -> p n (j d)", p=P, j=PACK
-                ),
+                in_=H_mean_A[first : first + ROUND_PASSES * K_PASS, :].rearrange("(n p j) d -> p n (j d)", p=P, j=PACK),
             )
             return hm_rows
 
@@ -118,42 +117,58 @@ def tile_mymodel_icdm_pa_k_kernel(tc, H_A, H_mean_A, H_mean_M, wEA1, bEA1, out):
             nc.sync.dma_start(out=bias_rows[0:1, :], in_=bEA1.rearrange("(o h) -> o h", o=1))
             return event_rows, w_rows
 
-        def prepare_small(w_rows):
-            w_grouped = consts.tile([P, H3, PACK], BF16, align_bytes=64)
-            regroup(nc.scalar.copy, w_grouped[:], w_rows[:])
-            bias_ps = psum_ring.tile([P, 4 * H3], F32, tag="out_ps")
-            nc.tensor.matmul(out=bias_ps[:, 0:H3], lhsT=ones[:], rhs=bias_rows[:], start=True, stop=True)
-            bias_all = consts.tile([P, H3], F32)
-            nc.vector.tensor_copy(out=bias_all[:], in_=bias_ps[:, 0:H3])
-            w = quantise(consts, "w", w_grouped[:].rearrange("p h j -> p (h j)"))
-            return w, bias_all
+        ha_rows_a = raw_pass.tile([P, PACK, EVENTS], BF16, tag="ha_rows")
+        hm_rows = raw_round.tile([P, ROUND_PASSES, PACK, HD], BF16, tag="hm_rows")
+        ha_halves = H_A[0:K_PASS, :].rearrange("(p j) e -> p j e", j=PACK)
+        hm_passes = H_mean_A[0 : ROUND_PASSES * K_PASS, :].rearrange("(n p j) d -> p n (j d)", p=P, j=PACK)
+        for n in range(ROUND_PASSES):
+            half = slice(n * EVENTS // 2, (n + 1) * EVENTS // 2)
+            nc.sync.dma_start(out=ha_rows_a[:, :, half], in_=ha_halves[:, :, half])
+            nc.sync.dma_start(out=hm_rows[:, n].rearrange("p j d -> p (j d)"), in_=hm_passes[:, n])
+        hm_grouped = work_round.tile([P, ROUND_PASSES, HD, PACK], BF16, tag="hm_grouped", align_bytes=64)
+        ha_grouped_a = work_pass.tile([P, EVENTS, PACK], BF16, tag="ha_grouped", align_bytes=64)
+        for n in range(ROUND_PASSES):
+            half = slice(n * EVENTS // 2, (n + 1) * EVENTS // 2)
+            regroup(nc.scalar.copy, ha_grouped_a[:, half, :], ha_rows_a[:, :, half])
+            regroup(nc.vector.tensor_copy, hm_grouped[:, n], hm_rows[:, n])
 
         for r in range(ROUNDS - 1):
             t = r * ROUND_PASSES
-            ha_rows_a = load_events(t)
-            hm_rows = load_features(t)
+            if r > 0:
+                ha_rows_a = load_events(t)
             ha_rows_b = load_events(t + 1)
+            hm_rows = load_features(r + 1)
             if r == SMALL_LOAD_ROUND:
                 event_rows, w_rows = load_small()
 
-            ha_grouped_a = work_pass.tile([P, EVENTS, PACK], BF16, tag="ha_grouped", align_bytes=64)
-            regroup(nc.scalar.copy, ha_grouped_a[:], ha_rows_a[:])
+            if r > 0:
+                ha_grouped_a = work_pass.tile([P, EVENTS, PACK], BF16, tag="ha_grouped", align_bytes=64)
+                regroup(nc.scalar.copy, ha_grouped_a[:], ha_rows_a[:])
             ha_grouped_b = work_pass.tile([P, EVENTS, PACK], BF16, tag="ha_grouped", align_bytes=64)
             regroup(nc.scalar.copy, ha_grouped_b[:, 0:SCALAR_COLS, :], ha_rows_b[:, :, 0:SCALAR_COLS])
 
-            hm_grouped = work_round.tile([P, ROUND_PASSES, HD, PACK], BF16, align_bytes=64)
-            regroup_passes(nc.vector.tensor_copy, hm_grouped[:], hm_rows[:])
-            ha_a = quantise(work_pass, "ha", ha_grouped_a[:].rearrange("p e j -> p (e j)"))
+            if r == 0:
+                hm = quantise(work_round, "hm", hm_grouped[:].rearrange("p n d j -> p (n d j)"))
             regroup(nc.vector.tensor_copy, ha_grouped_b[:, SCALAR_COLS:EVENTS, :], ha_rows_b[:, :, SCALAR_COLS:EVENTS])
-            hm = quantise(work_round, "hm", hm_grouped[:].rearrange("p n d j -> p (n d j)"))
+            ha_a = quantise(work_pass, "ha", ha_grouped_a[:].rearrange("p e j -> p (e j)"))
             multiply(t, ha_a[0], ha_a[1], hm[0], hm[1])
+            hm_grouped = work_round.tile([P, ROUND_PASSES, HD, PACK], BF16, tag="hm_grouped", align_bytes=64)
+            regroup_passes(nc.vector.tensor_copy, hm_grouped[:], hm_rows[:])
             ha_b = quantise(work_pass, "ha", ha_grouped_b[:].rearrange("p e j -> p (e j)"))
             multiply(t + 1, ha_b[0], ha_b[1], hm[0], hm[1])
+            hm = quantise(work_round, "hm", hm_grouped[:].rearrange("p n d j -> p (n d j)"))
+
             if r == SMALL_LOAD_ROUND + 1:
-                w, bias_all = prepare_small(w_rows)
+                w_grouped = consts.tile([P, H3, PACK], BF16, align_bytes=64)
+                regroup(nc.scalar.copy, w_grouped[:], w_rows[:])
+                bias_ps = psum_ring.tile([P, 4, H3], F32, tag="out_ps")
+                nc.tensor.matmul(out=bias_ps[:, 0, :], lhsT=ones[:], rhs=bias_rows[:], start=True, stop=True)
+            if r == SMALL_LOAD_ROUND + 2:
+                bias_all = consts.tile([P, H3], F32)
+                nc.vector.tensor_copy(out=bias_all[:], in_=bias_ps[:, 0, :])
+                w = quantise(consts, "w", w_grouped[:].rearrange("p h j -> p (h j)"))
 
         t = (ROUNDS - 1) * ROUND_PASSES
-        hm_rows = load_features(t)
         ha_rows = raw_pass.tile([P, ROUND_PASSES, PACK, EVENTS], BF16, name="ha_rows_last", tag="ha_rows_last", bufs=1)
         for n in range(ROUND_PASSES):
             nc.sync.dma_start(
@@ -206,10 +221,9 @@ def tile_mymodel_icdm_pa_k_kernel(tc, H_A, H_mean_A, H_mean_M, wEA1, bEA1, out):
         def tile_fused(a):
             return quantise(work_round, "fused", fused_grouped[:, a].rearrange("p e j -> p (e j)"))
 
-        def tile_out(codes, scales):
-            out_ps = psum_ring.tile([P, 4 * H3], F32, tag="out_ps")
+        def tile_out(out_ps, a, codes, scales):
             nc.tensor.matmul_mx(
-                out=out_ps[:, 0:H3],
+                out=out_ps[:, a % 2, :],
                 lhsT=codes[:].bitcast(FP8X4),
                 lhsT_scale=scales[:],
                 rhs=w[0][:].bitcast(FP8X4),
@@ -217,13 +231,18 @@ def tile_mymodel_icdm_pa_k_kernel(tc, H_A, H_mean_A, H_mean_M, wEA1, bEA1, out):
                 start=True,
                 stop=True,
             )
-            return out_ps
 
-        def tile_bias(a, out_ps):
-            nc.vector.tensor_tensor(out=result[:, a, :], in0=out_ps[:, 0:H3], in1=bias_all[:], op=ADD)
+        def add_bias(out_ps, first, last):
+            count = last - first
+            nc.vector.tensor_tensor(
+                out=result[:, first:last, :],
+                in0=out_ps[:, first % 2 : first % 2 + count, :],
+                in1=bias_all[:].unsqueeze(1).to_broadcast([P, count, H3]),
+                op=ADD,
+            )
 
-        def tile_relu(a):
-            nc.scalar.activation(out=result[:, a, :], in_=result[:, a, :], func=RELU)
+        def relu(first, last):
+            nc.scalar.activation(out=result[:, first:last, :], in_=result[:, first:last, :], func=RELU)
 
         def store(first, last):
             nc.sync.dma_start(
@@ -232,49 +251,42 @@ def tile_mymodel_icdm_pa_k_kernel(tc, H_A, H_mean_A, H_mean_M, wEA1, bEA1, out):
 
         v_copy = nc.vector.tensor_copy
         s_copy = nc.scalar.copy
-        hm_grouped = work_round.tile([P, ROUND_PASSES, HD, PACK], BF16, align_bytes=64)
-        regroup_passes(v_copy, hm_grouped[:], hm_rows[:])
         tile_copy(s_copy, 0)
-        tile_copy(v_copy, 2)
-        hm = quantise(work_round, "hm", hm_grouped[:].rearrange("p n d j -> p (n d j)"))
-        q0 = tile_quantise(0)
-        tile_multiply(0, *q0)
         tile_copy(s_copy, 1)
-        q2 = tile_quantise(2)
-        tile_multiply(2, *q2)
-        tile_copy(v_copy, 3, P // 2, P)
+        tile_copy(s_copy, 2, 0, P // 2)
         tile_copy(s_copy, 3, 0, P // 2)
-        q1 = tile_quantise(1)
-        tile_multiply(1, *q1)
-        tile_sum(v_copy, 0)
+        tile_copy(v_copy, 3, P // 2, P)
+        tile_copy(v_copy, 2, P // 2, P)
+        tile_multiply(0, *tile_quantise(0))
+        tile_multiply(1, *tile_quantise(1))
+        tile_sum(s_copy, 0)
         wt0 = tile_transpose(0)
-        q3 = tile_quantise(3)
-        tile_multiply(3, *q3)
+        tile_multiply(2, *tile_quantise(2))
+        tile_sum(s_copy, 1)
+        wt1 = tile_transpose(1)
+        tile_multiply(3, *tile_quantise(3))
+        tile_interleave(s_copy, 0, wt0)
+        fused0 = tile_fused(0)
         tile_sum(s_copy, 2)
         wt2 = tile_transpose(2)
-        tile_sum(s_copy, 1)
-        tile_interleave(v_copy, 0, wt0)
-        wt1 = tile_transpose(1)
-        tile_interleave(s_copy, 2, wt2)
+        tile_interleave(s_copy, 1, wt1)
         tile_sum(v_copy, 3)
         wt3 = tile_transpose(3)
-        f0 = tile_fused(0)
-        o0 = tile_out(*f0)
-        tile_interleave(s_copy, 1, wt1)
-        f2 = tile_fused(2)
-        o2 = tile_out(*f2)
-        tile_bias(0, o0)
-        tile_relu(0)
-        tile_interleave(v_copy, 3, wt3)
-        f1 = tile_fused(1)
-        o1 = tile_out(*f1)
-        f3 = tile_fused(3)
-        o3 = tile_out(*f3)
-        tile_bias(2, o2)
-        tile_relu(2)
-        tile_bias(1, o1)
-        tile_relu(1)
+        out01 = psum_ring.tile([P, 4, H3], F32, name="out01", tag="out_ps")
+        tile_out(out01, 0, *fused0)
+        tile_out(out01, 1, *tile_fused(1))
+        tile_interleave(s_copy, 2, wt2)
+        out2 = psum_ring.tile([P, 4, H3], F32, name="out2", tag="out_ps")
+        tile_out(out2, 2, *tile_fused(2))
+        tile_interleave(s_copy, 3, wt3)
+        add_bias(out01, 0, 2)
+        fused3 = tile_fused(3)
+        out3 = psum_ring.tile([P, 4, H3], F32, name="out3", tag="out_ps")
+        tile_out(out3, 3, *fused3)
+        relu(0, 2)
+        add_bias(out2, 2, 3)
+        relu(2, 3)
         store(0, 3)
-        tile_bias(3, o3)
-        tile_relu(3)
+        add_bias(out3, 3, 4)
+        relu(3, 4)
         store(3, 4)

@@ -25,6 +25,10 @@ ROUNDS = PASSES // ROUND_PASSES
 
 SCALAR_COLS = 288
 
+FIRST_THRU_ROUND = 3
+THRU_COLS = 256
+THRU_SCALAR_COLS = 352
+
 RUN = 4
 
 SMALL_LOAD_ROUND = 4
@@ -70,6 +74,8 @@ def tile_mymodel_icdm_pa_k_kernel(tc, H_A, H_mean_A, H_mean_M, wEA1, bEA1, out):
 
         identity = consts.tile([P, P], F32)
         make_identity(nc, identity[:])
+        identity_bf = consts.tile([P, P], BF16)
+        make_identity(nc, identity_bf[:])
         ones = consts.tile([P, P], BF16)
         nc.vector.memset(ones[:], 1.0)
         bias_rows = consts.tile([P, H3], BF16)
@@ -141,21 +147,38 @@ def tile_mymodel_icdm_pa_k_kernel(tc, H_A, H_mean_A, H_mean_M, wEA1, bEA1, out):
             if r == SMALL_LOAD_ROUND:
                 event_rows, w_rows = load_small()
 
+            thru = r >= FIRST_THRU_ROUND
+            if thru:
+                thru_ps = psum_ring.tile([P, THRU_COLS, PACK], BF16, tag="word_t")
+                for j in range(0, PACK, 2):
+                    nc.tensor.matmul(
+                        out=thru_ps[:, :, j : j + 2].rearrange("p e j -> p j e"),
+                        lhsT=identity_bf[:],
+                        rhs=ha_rows_b[:, j : j + 2, 0:THRU_COLS],
+                        start=True,
+                        stop=True,
+                    )
+            if r > 0:
+                multiply(t - 1, ha_b[0], ha_b[1], hm_before[0], hm_before[1])
+
             if r > 0:
                 ha_grouped_a = work_pass.tile([P, EVENTS, PACK], BF16, tag="ha_grouped", align_bytes=64)
                 regroup(nc.scalar.copy, ha_grouped_a[:], ha_rows_a[:])
             ha_grouped_b = work_pass.tile([P, EVENTS, PACK], BF16, tag="ha_grouped", align_bytes=64)
-            regroup(nc.scalar.copy, ha_grouped_b[:, 0:SCALAR_COLS, :], ha_rows_b[:, :, 0:SCALAR_COLS])
+            first, last = (THRU_COLS, THRU_SCALAR_COLS) if thru else (0, SCALAR_COLS)
+            regroup(nc.scalar.copy, ha_grouped_b[:, first:last, :], ha_rows_b[:, :, first:last])
+            if thru:
+                nc.scalar.copy(out=ha_grouped_b[:, 0:THRU_COLS, :], in_=thru_ps[:])
 
             if r == 0:
                 hm = quantise(work_round, "hm", hm_grouped[:].rearrange("p n d j -> p (n d j)"))
-            regroup(nc.vector.tensor_copy, ha_grouped_b[:, SCALAR_COLS:EVENTS, :], ha_rows_b[:, :, SCALAR_COLS:EVENTS])
+            regroup(nc.vector.tensor_copy, ha_grouped_b[:, last:EVENTS, :], ha_rows_b[:, :, last:EVENTS])
             ha_a = quantise(work_pass, "ha", ha_grouped_a[:].rearrange("p e j -> p (e j)"))
             multiply(t, ha_a[0], ha_a[1], hm[0], hm[1])
             hm_grouped = work_round.tile([P, ROUND_PASSES, HD, PACK], BF16, tag="hm_grouped", align_bytes=64)
             regroup_passes(nc.vector.tensor_copy, hm_grouped[:], hm_rows[:])
             ha_b = quantise(work_pass, "ha", ha_grouped_b[:].rearrange("p e j -> p (e j)"))
-            multiply(t + 1, ha_b[0], ha_b[1], hm[0], hm[1])
+            hm_before = hm
             hm = quantise(work_round, "hm", hm_grouped[:].rearrange("p n d j -> p (n d j)"))
 
             if r == SMALL_LOAD_ROUND + 1:
@@ -169,6 +192,7 @@ def tile_mymodel_icdm_pa_k_kernel(tc, H_A, H_mean_A, H_mean_M, wEA1, bEA1, out):
                 w = quantise(consts, "w", w_grouped[:].rearrange("p h j -> p (h j)"))
 
         t = (ROUNDS - 1) * ROUND_PASSES
+        multiply(t - 1, ha_b[0], ha_b[1], hm_before[0], hm_before[1])
         ha_rows = raw_pass.tile([P, ROUND_PASSES, PACK, EVENTS], BF16, name="ha_rows_last", tag="ha_rows_last", bufs=1)
         for n in range(ROUND_PASSES):
             nc.sync.dma_start(

@@ -115,37 +115,25 @@ def tile_mymodel_icdm_pa_k_kernel(tc, H_A, H_mean_A, H_mean_M, wEA1, bEA1, out):
                     stop=False,
                 )
 
-        def load_small():
-            event_rows = consts.tile([P, EVENT_TILES, FUSED], BF16)
-            nc.sync.dma_start(out=event_rows[:, :, 0:HD], in_=H_mean_M.rearrange("(a p) c -> p a c", p=P))
-            w_rows = consts.tile([P, PACK, H3], BF16)
-            nc.sync.dma_start(out=w_rows[:], in_=wEA1.rearrange("(p j) h -> p j h", j=PACK))
-            nc.sync.dma_start(out=bias_rows[0:1, :], in_=bEA1.rearrange("(o h) -> o h", o=1))
-            return event_rows, w_rows
-
-        ha_rows_a = raw_pass.tile([P, PACK, EVENTS], BF16, tag="ha_rows")
         hm_rows = raw_round.tile([P, ROUND_PASSES, PACK, HD], BF16, tag="hm_rows")
-        ha_halves = H_A[0:K_PASS, :].rearrange("(p j) e -> p j e", j=PACK)
         hm_passes = H_mean_A[0 : ROUND_PASSES * K_PASS, :].rearrange("(n p j) d -> p n (j d)", p=P, j=PACK)
-        for n in range(ROUND_PASSES):
-            half = slice(n * EVENTS // 2, (n + 1) * EVENTS // 2)
-            nc.sync.dma_start(out=ha_rows_a[:, :, half], in_=ha_halves[:, :, half])
-            nc.sync.dma_start(out=hm_rows[:, n].rearrange("p j d -> p (j d)"), in_=hm_passes[:, n])
         hm_grouped = work_round.tile([P, ROUND_PASSES, HD, PACK], BF16, tag="hm_grouped", align_bytes=64)
-        ha_grouped_a = work_pass.tile([P, EVENTS, PACK], BF16, tag="ha_grouped", align_bytes=64)
+        ha_rows_of = {}
         for n in range(ROUND_PASSES):
-            half = slice(n * EVENTS // 2, (n + 1) * EVENTS // 2)
-            regroup(nc.scalar.copy, ha_grouped_a[:, half, :], ha_rows_a[:, :, half])
+            nc.sync.dma_start(out=hm_rows[:, n].rearrange("p j d -> p (j d)"), in_=hm_passes[:, n])
+            ha_rows_of[n] = load_events(n)
             regroup(nc.vector.tensor_copy, hm_grouped[:, n], hm_rows[:, n])
 
         for r in range(ROUNDS - 1):
             t = r * ROUND_PASSES
             if r > 0:
-                ha_rows_a = load_events(t)
-            ha_rows_b = load_events(t + 1)
+                ha_rows_of = {n: load_events(t + n) for n in range(ROUND_PASSES)}
+            ha_rows_a, ha_rows_b = ha_rows_of[0], ha_rows_of[1]
             hm_rows = load_features(r + 1)
             if r == SMALL_LOAD_ROUND:
-                event_rows, w_rows = load_small()
+                w_rows = consts.tile([P, PACK, H3], BF16)
+                nc.sync.dma_start(out=w_rows[:], in_=wEA1.rearrange("(p j) h -> p j h", j=PACK))
+                nc.sync.dma_start(out=bias_rows[0:1, :], in_=bEA1.rearrange("(o h) -> o h", o=1))
 
             thru = r >= FIRST_THRU_ROUND
             if thru:
@@ -161,9 +149,8 @@ def tile_mymodel_icdm_pa_k_kernel(tc, H_A, H_mean_A, H_mean_M, wEA1, bEA1, out):
             if r > 0:
                 multiply(t - 1, ha_b[0], ha_b[1], hm_before[0], hm_before[1])
 
-            if r > 0:
-                ha_grouped_a = work_pass.tile([P, EVENTS, PACK], BF16, tag="ha_grouped", align_bytes=64)
-                regroup(nc.scalar.copy, ha_grouped_a[:], ha_rows_a[:])
+            ha_grouped_a = work_pass.tile([P, EVENTS, PACK], BF16, tag="ha_grouped", align_bytes=64)
+            regroup(nc.scalar.copy, ha_grouped_a[:], ha_rows_a[:])
             ha_grouped_b = work_pass.tile([P, EVENTS, PACK], BF16, tag="ha_grouped", align_bytes=64)
             first, last = (THRU_COLS, THRU_SCALAR_COLS) if thru else (0, SCALAR_COLS)
             regroup(nc.scalar.copy, ha_grouped_b[:, first:last, :], ha_rows_b[:, :, first:last])
@@ -192,38 +179,51 @@ def tile_mymodel_icdm_pa_k_kernel(tc, H_A, H_mean_A, H_mean_M, wEA1, bEA1, out):
                 w = quantise(consts, "w", w_grouped[:].rearrange("p h j -> p (h j)"))
 
         t = (ROUNDS - 1) * ROUND_PASSES
+        ha_rows_a = load_events(t)
+        ha_rows_b = load_events(t + 1)
+        event_rows = consts.tile([P, EVENT_TILES, FUSED], BF16)
+        nc.sync.dma_start(out=event_rows[:, :, 0:HD], in_=H_mean_M.rearrange("(a p) c -> p a c", p=P))
+
         multiply(t - 1, ha_b[0], ha_b[1], hm_before[0], hm_before[1])
-        ha_rows = raw_pass.tile([P, ROUND_PASSES, PACK, EVENTS], BF16, name="ha_rows_last", tag="ha_rows_last", bufs=1)
-        for n in range(ROUND_PASSES):
-            nc.sync.dma_start(
-                out=ha_rows[:, n].rearrange("p j e -> p (j e)"),
-                in_=H_A[(t + n) * K_PASS : (t + n + 1) * K_PASS, :].rearrange("(p j) e -> p (j e)", j=PACK),
-            )
-        tile_grouped = consts.tile([P, EVENT_TILES, ROUND_PASSES, P, PACK], BF16, align_bytes=64)
+        halves = []
+        for h, copy in enumerate((nc.scalar.copy, nc.vector.tensor_copy)):
+            half_grouped = work_pass.tile([P, EVENTS // 2, PACK], BF16, align_bytes=64)
+            regroup(copy, half_grouped[:], ha_rows_a[:, :, h * EVENTS // 2 : (h + 1) * EVENTS // 2])
+            halves.append(half_grouped)
+
+        tile_grouped = consts.tile([P, EVENT_TILES, P, PACK], BF16, align_bytes=64)
         fused_grouped = consts.tile([P, EVENT_TILES, P, PACK], BF16, align_bytes=64)
         result = consts.tile([P, EVENT_TILES, H3], F32)
         words = event_rows[:].rearrange("p a c -> p (a c)").bitcast(F32)
         event_words = FUSED // 2
 
-        def tile_copy(copy, a, first=0, last=P):
-            regroup_passes(
-                copy, tile_grouped[:, a, :, first:last, :], ha_rows[:, :, :, a * P + first : a * P + last]
-            )
-
-        def tile_quantise(a):
-            return quantise(work_round, "tile", tile_grouped[:, a].rearrange("p n e j -> p (n e j)"))
-
-        def tile_multiply(a, codes, scales):
-            for n in range(ROUND_PASSES):
+        def half_multiply(h):
+            codes, scales = quantise(work_pass, "half", halves[h][:].rearrange("p e j -> p (e j)"))
+            for i in range(EVENT_TILES // 2):
                 nc.tensor.matmul_mx(
-                    out=sums[a][:, 0:HD],
-                    lhsT=codes[:, n * P : (n + 1) * P].bitcast(FP8X4),
-                    lhsT_scale=scales[:, n * P : (n + 1) * P],
-                    rhs=hm[0][:, n * HD : (n + 1) * HD].bitcast(FP8X4),
-                    rhs_scale=hm[1][:, n * HD : (n + 1) * HD],
+                    out=sums[h * EVENT_TILES // 2 + i][:, 0:HD],
+                    lhsT=codes[:, i * P : (i + 1) * P].bitcast(FP8X4),
+                    lhsT_scale=scales[:, i * P : (i + 1) * P],
+                    rhs=hm[0][:, 0:HD].bitcast(FP8X4),
+                    rhs_scale=hm[1][:, 0:HD],
                     start=False,
-                    stop=(n == ROUND_PASSES - 1),
+                    stop=False,
                 )
+
+        def tile_copy(copy, a):
+            regroup(copy, tile_grouped[:, a], ha_rows_b[:, :, a * P : (a + 1) * P])
+
+        def tile_multiply(a):
+            codes, scales = quantise(work_round, "tile", tile_grouped[:, a].rearrange("p e j -> p (e j)"))
+            nc.tensor.matmul_mx(
+                out=sums[a][:, 0:HD],
+                lhsT=codes[:].bitcast(FP8X4),
+                lhsT_scale=scales[:],
+                rhs=hm[0][:, HD : 2 * HD].bitcast(FP8X4),
+                rhs_scale=hm[1][:, HD : 2 * HD],
+                start=False,
+                stop=True,
+            )
 
         def tile_sum(copy, a):
             copy(out=event_rows[:, a, HD:FUSED], in_=sums[a][:, 0:HD])
@@ -245,9 +245,9 @@ def tile_mymodel_icdm_pa_k_kernel(tc, H_A, H_mean_A, H_mean_M, wEA1, bEA1, out):
         def tile_fused(a):
             return quantise(work_round, "fused", fused_grouped[:, a].rearrange("p e j -> p (e j)"))
 
-        def tile_out(out_ps, a, codes, scales):
+        def tile_out(out_ps, slot, codes, scales):
             nc.tensor.matmul_mx(
-                out=out_ps[:, a % 2, :],
+                out=out_ps[:, slot, :],
                 lhsT=codes[:].bitcast(FP8X4),
                 lhsT_scale=scales[:],
                 rhs=w[0][:].bitcast(FP8X4),
@@ -256,17 +256,16 @@ def tile_mymodel_icdm_pa_k_kernel(tc, H_A, H_mean_A, H_mean_M, wEA1, bEA1, out):
                 stop=True,
             )
 
-        def add_bias(out_ps, first, last):
-            count = last - first
+        def add_bias(a, out_ps, slot, count=1):
             nc.vector.tensor_tensor(
-                out=result[:, first:last, :],
-                in0=out_ps[:, first % 2 : first % 2 + count, :],
+                out=result[:, a : a + count, :],
+                in0=out_ps[:, slot : slot + count, :],
                 in1=bias_all[:].unsqueeze(1).to_broadcast([P, count, H3]),
                 op=ADD,
             )
 
-        def relu(first, last):
-            nc.scalar.activation(out=result[:, first:last, :], in_=result[:, first:last, :], func=RELU)
+        def relu(a, count=1):
+            nc.scalar.activation(out=result[:, a : a + count, :], in_=result[:, a : a + count, :], func=RELU)
 
         def store(first, last):
             nc.sync.dma_start(
@@ -275,42 +274,39 @@ def tile_mymodel_icdm_pa_k_kernel(tc, H_A, H_mean_A, H_mean_M, wEA1, bEA1, out):
 
         v_copy = nc.vector.tensor_copy
         s_copy = nc.scalar.copy
-        tile_copy(s_copy, 0)
-        tile_copy(s_copy, 1)
-        tile_copy(s_copy, 2, 0, P // 2)
-        tile_copy(s_copy, 3, 0, P // 2)
-        tile_copy(v_copy, 3, P // 2, P)
-        tile_copy(v_copy, 2, P // 2, P)
-        tile_multiply(0, *tile_quantise(0))
-        tile_multiply(1, *tile_quantise(1))
+        half_multiply(1)
+        half_multiply(0)
+        tile_copy(s_copy, 2)
+        tile_copy(s_copy, 3)
+        tile_copy(v_copy, 0)
+        tile_copy(v_copy, 1)
+        tile_multiply(0)
+        tile_multiply(2)
         tile_sum(s_copy, 0)
-        wt0 = tile_transpose(0)
-        tile_multiply(2, *tile_quantise(2))
-        tile_sum(s_copy, 1)
-        wt1 = tile_transpose(1)
-        tile_multiply(3, *tile_quantise(3))
-        tile_interleave(s_copy, 0, wt0)
-        fused0 = tile_fused(0)
+        tile_multiply(1)
+        tile_multiply(3)
         tile_sum(s_copy, 2)
+        wt0 = tile_transpose(0)
+        tile_sum(v_copy, 1)
         wt2 = tile_transpose(2)
-        tile_interleave(s_copy, 1, wt1)
         tile_sum(v_copy, 3)
-        wt3 = tile_transpose(3)
-        out01 = psum_ring.tile([P, 4, H3], F32, name="out01", tag="out_ps")
-        tile_out(out01, 0, *fused0)
-        tile_out(out01, 1, *tile_fused(1))
+        tile_interleave(s_copy, 0, wt0)
+        wt1 = tile_transpose(1)
         tile_interleave(s_copy, 2, wt2)
-        out2 = psum_ring.tile([P, 4, H3], F32, name="out2", tag="out_ps")
-        tile_out(out2, 2, *tile_fused(2))
+        wt3 = tile_transpose(3)
+        out_a = psum_ring.tile([P, 4, H3], F32, name="out_a", tag="out_ps")
+        out_b = psum_ring.tile([P, 4, H3], F32, name="out_b", tag="out_ps")
+        tile_out(out_a, 0, *tile_fused(0))
+        tile_interleave(v_copy, 1, wt1)
+        fused2 = tile_fused(2)
         tile_interleave(s_copy, 3, wt3)
-        add_bias(out01, 0, 2)
+        tile_out(out_a, 1, *tile_fused(1))
+        tile_out(out_b, 0, *fused2)
+        add_bias(0, out_a, 0, 2)
         fused3 = tile_fused(3)
-        out3 = psum_ring.tile([P, 4, H3], F32, name="out3", tag="out_ps")
-        tile_out(out3, 3, *fused3)
+        tile_out(out_b, 1, *fused3)
         relu(0, 2)
-        add_bias(out2, 2, 3)
-        relu(2, 3)
-        store(0, 3)
-        add_bias(out3, 3, 4)
-        relu(3, 4)
-        store(3, 4)
+        store(0, 2)
+        add_bias(2, out_b, 0, 2)
+        relu(2, 2)
+        store(2, 4)

@@ -17,36 +17,30 @@ K_PASS = P * PACK
 
 NODES, EVENTS, HD, H3 = 16384, 512, 256, 128
 FUSED = 2 * HD
+EVENT_WORDS = FUSED // 2
 EVENT_TILES = EVENTS // P
 PASSES = NODES // K_PASS
 
-ROUND_PASSES = 2
-ROUNDS = PASSES // ROUND_PASSES
+SINGLE_PASSES = 4
+TAIL_PASSES = 4
 
-SCALAR_COLS = 288
+SCALAR_COLS = {EVENTS: EVENTS // 2, HD: HD // 2}
 
-FIRST_THRU_ROUND = 3
-THRU_COLS = 256
-THRU_SCALAR_COLS = 352
+TENSOR_COLS = 128
+SCALAR_COLS_BESIDE = 296
 
 RUN = 4
 
-SMALL_LOAD_ROUND = 4
+SMALL_LOAD_CHUNK = 9
 
-RAW_ROUNDS = 8
-WORK_ROUNDS = 3
+ROWS_BUFS = {(HD, 1): 2, (HD, 2): 2, (HD, 4): 3, (EVENTS, 1): 6, (EVENTS, 2): 5}
+GROUPED_BUFS = {(HD, 1): 2, (HD, 2): 2, (HD, 4): 2, (EVENTS, 1): 3, (EVENTS, 2): 3}
+CODES_BUFS = 3
 
 FLOPS = 2 * NODES * EVENTS * HD + 2 * EVENTS * FUSED * H3
 
 
 def regroup(copy, grouped, rows):
-    copy(
-        out=grouped.rearrange("p (c i) j -> p c j i", i=RUN),
-        in_=rows.rearrange("p j (c i) -> p c j i", i=RUN),
-    )
-
-
-def regroup_passes(copy, grouped, rows):
     copy(
         out=grouped.rearrange("p n (c i) j -> p n c j i", i=RUN),
         in_=rows.rearrange("p n j (c i) -> p n c j i", i=RUN),
@@ -55,20 +49,20 @@ def regroup_passes(copy, grouped, rows):
 
 def tile_mymodel_icdm_pa_k_kernel(tc, H_A, H_mean_A, H_mean_M, wEA1, bEA1, out):
     nc = tc.nc
+    v_copy = nc.vector.tensor_copy
+    s_copy = nc.scalar.copy
     with ExitStack() as stack:
         consts = stack.enter_context(tc.tile_pool(name="consts", bufs=1))
-        raw_pass = stack.enter_context(tc.tile_pool(name="raw_pass", bufs=RAW_ROUNDS * ROUND_PASSES))
-        raw_round = stack.enter_context(tc.tile_pool(name="raw_round", bufs=RAW_ROUNDS))
-        work_pass = stack.enter_context(tc.tile_pool(name="work_pass", bufs=WORK_ROUNDS * ROUND_PASSES))
-        work_round = stack.enter_context(tc.tile_pool(name="work_round", bufs=WORK_ROUNDS))
+        raw = stack.enter_context(tc.tile_pool(name="raw", bufs=2))
+        work = stack.enter_context(tc.tile_pool(name="work", bufs=2))
         psum = stack.enter_context(tc.psum_pool(name="psum", bufs=1))
         psum_ring = stack.enter_context(tc.psum_pool(name="psum_ring", bufs=2))
         stack.enter_context(tc.manual_schedule())
 
-        def quantise(pool, name, grouped):
+        def quantise(name, grouped, bufs):
             words = grouped.shape[1] // PACK
-            codes = pool.tile([P, words], U32, name=name + "_codes", tag=name + "_codes", align_bytes=64)
-            scales = pool.tile([P, words], U8, name=name + "_scales", tag=name + "_scales", align_bytes=64)
+            codes = work.tile([P, words], U32, name=name + "_codes", tag=name + "_codes", bufs=bufs, align_bytes=64)
+            scales = work.tile([P, words], U8, name=name + "_scales", tag=name + "_scales", bufs=bufs, align_bytes=64)
             nc.vector.quantize_mx(out=codes[:].bitcast(FP8X4), scales=scales[:], in_=grouped)
             return codes, scales
 
@@ -82,172 +76,146 @@ def tile_mymodel_icdm_pa_k_kernel(tc, H_A, H_mean_A, H_mean_M, wEA1, bEA1, out):
         nc.vector.memset(bias_rows[:], 0.0)
 
         sums = [psum.tile([P, 2 * HD], F32, name="sum%d" % a) for a in range(EVENT_TILES)]
+        features = {}
 
-        def load_events(t):
-            ha_rows = raw_pass.tile([P, PACK, EVENTS], BF16)
+        def load(source, t, passes):
+            width = source.shape[1]
+            name = "rows_%d_%d" % (width, passes)
+            rows = raw.tile([P, passes, PACK, width], BF16, name=name, tag=name, bufs=ROWS_BUFS[(width, passes)])
             nc.sync.dma_start(
-                out=ha_rows[:].rearrange("p j e -> p (j e)"),
-                in_=H_A[t * K_PASS : (t + 1) * K_PASS, :].rearrange("(p j) e -> p (j e)", j=PACK),
+                out=rows[:].rearrange("p n j w -> p n (j w)"),
+                in_=source[t * K_PASS : (t + passes) * K_PASS, :].rearrange("(n p j) w -> p n (j w)", p=P, j=PACK),
             )
-            return ha_rows
+            return rows[:]
 
-        def load_features(r):
-            hm_rows = raw_round.tile([P, ROUND_PASSES, PACK, HD], BF16)
-            first = r * ROUND_PASSES * K_PASS
-            nc.sync.dma_start(
-                out=hm_rows[:].rearrange("p n j d -> p n (j d)"),
-                in_=H_mean_A[first : first + ROUND_PASSES * K_PASS, :].rearrange("(n p j) d -> p n (j d)", p=P, j=PACK),
+        def tensor_regroup(rows):
+            bank = psum_ring.tile([P, 2, TENSOR_COLS, PACK], BF16, name="regrouped")
+            for n in range(2):
+                nc.tensor.matmul(
+                    out=bank[:, n].rearrange("p w j -> p j w"),
+                    lhsT=identity_bf[:],
+                    rhs=rows[:, n, :, 0:TENSOR_COLS],
+                    start=True,
+                    stop=True,
+                )
+            return bank
+
+        def copies(width, passes, rows, bank):
+            name = "grouped_%d_%d" % (width, passes)
+            grouped = work.tile(
+                [P, passes, width, PACK], BF16, name=name, tag=name, bufs=GROUPED_BUFS[(width, passes)], align_bytes=64
             )
-            return hm_rows
+            first, last = (0, SCALAR_COLS[width]) if bank is None else (TENSOR_COLS, SCALAR_COLS_BESIDE)
+            regroup(s_copy, grouped[:, :, first:last], rows[:, :, :, first:last])
+            if bank is not None:
+                s_copy(
+                    out=grouped[:, :, 0:TENSOR_COLS].rearrange("p n w j -> p n (w j)"),
+                    in_=bank[:].rearrange("p n w j -> p n (w j)"),
+                )
+            regroup(v_copy, grouped[:, :, last:width], rows[:, :, :, last:width])
+            return grouped
 
-        def multiply(t, ha_codes, ha_scales, hm_codes, hm_scales):
-            first = (t % ROUND_PASSES) * HD
-            features = slice(first, first + HD)
-            for a in range(EVENT_TILES):
-                events = slice(a * P, (a + 1) * P)
+        def multiply(t, codes, scales, tiles, stop):
+            for i, a in enumerate(tiles):
                 nc.tensor.matmul_mx(
                     out=sums[a][:, 0:HD],
-                    lhsT=ha_codes[:, events].bitcast(FP8X4),
-                    lhsT_scale=ha_scales[:, events],
-                    rhs=hm_codes[:, features].bitcast(FP8X4),
-                    rhs_scale=hm_scales[:, features],
+                    lhsT=codes[:, i * P : (i + 1) * P].bitcast(FP8X4),
+                    lhsT_scale=scales[:, i * P : (i + 1) * P],
+                    rhs=features[t][0].bitcast(FP8X4),
+                    rhs_scale=features[t][1],
                     start=(t == 0),
-                    stop=False,
+                    stop=stop,
                 )
 
-        hm_rows = raw_round.tile([P, ROUND_PASSES, PACK, HD], BF16, tag="hm_rows")
-        hm_passes = H_mean_A[0 : ROUND_PASSES * K_PASS, :].rearrange("(n p j) d -> p n (j d)", p=P, j=PACK)
-        hm_grouped = work_round.tile([P, ROUND_PASSES, HD, PACK], BF16, tag="hm_grouped", align_bytes=64)
-        ha_rows_of = {}
-        for n in range(ROUND_PASSES):
-            nc.sync.dma_start(out=hm_rows[:, n].rearrange("p j d -> p (j d)"), in_=hm_passes[:, n])
-            ha_rows_of[n] = load_events(n)
-            regroup(nc.vector.tensor_copy, hm_grouped[:, n], hm_rows[:, n])
+        def finish(source, t, passes, grouped):
+            width = source.shape[1]
+            codes, scales = quantise(
+                "chunk_%d_%d" % (width, passes), grouped[:].rearrange("p n w j -> p (n w j)"), CODES_BUFS
+            )
+            for n in range(passes):
+                cols = slice(n * width, (n + 1) * width)
+                if width == HD:
+                    features[t + n] = (codes[:, cols], scales[:, cols])
+                else:
+                    multiply(t + n, codes[:, cols], scales[:, cols], range(EVENT_TILES), False)
 
-        for r in range(ROUNDS - 1):
-            t = r * ROUND_PASSES
-            if r > 0:
-                ha_rows_of = {n: load_events(t + n) for n in range(ROUND_PASSES)}
-            ha_rows_a, ha_rows_b = ha_rows_of[0], ha_rows_of[1]
-            hm_rows = load_features(r + 1)
-            if r == SMALL_LOAD_ROUND:
-                w_rows = consts.tile([P, PACK, H3], BF16)
-                nc.sync.dma_start(out=w_rows[:], in_=wEA1.rearrange("(p j) h -> p j h", j=PACK))
+        chunks = [(H_mean_A, 0, 1, False), (H_mean_A, 1, 1, False), (H_A, 0, 1, False), (H_A, 1, 1, False)]
+        for t in range(2, SINGLE_PASSES, 2):
+            chunks += [(H_mean_A, t, 2, False), (H_A, t, 1, False), (H_A, t + 1, 1, False)]
+        for t in range(SINGLE_PASSES, PASSES - TAIL_PASSES, 4):
+            chunks += [(H_mean_A, t, 4, False), (H_A, t, 2, True), (H_A, t + 2, 2, True)]
+        chunks += [(H_mean_A, PASSES - TAIL_PASSES, TAIL_PASSES, False)]
+        chunks += [(H_A, t, 1, False) for t in range(PASSES - TAIL_PASSES, PASSES - 1)]
+
+        def fetch(i):
+            source, t, passes, shared = chunks[i]
+            rows = load(source, t, passes)
+            return rows, tensor_regroup(rows) if shared else None
+
+        fetched = fetch(0)
+        copied = None
+        for i, (source, t, passes, shared) in enumerate(chunks):
+            rows, bank = fetched
+            if i + 1 < len(chunks):
+                fetched = fetch(i + 1)
+            if i == SMALL_LOAD_CHUNK:
+                w_rows = consts.tile([P, 1, PACK, H3], BF16)
+                nc.sync.dma_start(
+                    out=w_rows[:].rearrange("p n j h -> p (n j) h"), in_=wEA1.rearrange("(p j) h -> p j h", j=PACK)
+                )
                 nc.sync.dma_start(out=bias_rows[0:1, :], in_=bEA1.rearrange("(o h) -> o h", o=1))
-
-            thru = r >= FIRST_THRU_ROUND
-            if thru:
-                thru_ps = psum_ring.tile([P, THRU_COLS, PACK], BF16, tag="word_t")
-                for j in range(0, PACK, 2):
-                    nc.tensor.matmul(
-                        out=thru_ps[:, :, j : j + 2].rearrange("p e j -> p j e"),
-                        lhsT=identity_bf[:],
-                        rhs=ha_rows_b[:, j : j + 2, 0:THRU_COLS],
-                        start=True,
-                        stop=True,
-                    )
-            if r > 0:
-                multiply(t - 1, ha_b[0], ha_b[1], hm_before[0], hm_before[1])
-
-            ha_grouped_a = work_pass.tile([P, EVENTS, PACK], BF16, tag="ha_grouped", align_bytes=64)
-            regroup(nc.scalar.copy, ha_grouped_a[:], ha_rows_a[:])
-            ha_grouped_b = work_pass.tile([P, EVENTS, PACK], BF16, tag="ha_grouped", align_bytes=64)
-            first, last = (THRU_COLS, THRU_SCALAR_COLS) if thru else (0, SCALAR_COLS)
-            regroup(nc.scalar.copy, ha_grouped_b[:, first:last, :], ha_rows_b[:, :, first:last])
-            if thru:
-                nc.scalar.copy(out=ha_grouped_b[:, 0:THRU_COLS, :], in_=thru_ps[:])
-
-            if r == 0:
-                hm = quantise(work_round, "hm", hm_grouped[:].rearrange("p n d j -> p (n d j)"))
-            regroup(nc.vector.tensor_copy, ha_grouped_b[:, last:EVENTS, :], ha_rows_b[:, :, last:EVENTS])
-            ha_a = quantise(work_pass, "ha", ha_grouped_a[:].rearrange("p e j -> p (e j)"))
-            multiply(t, ha_a[0], ha_a[1], hm[0], hm[1])
-            hm_grouped = work_round.tile([P, ROUND_PASSES, HD, PACK], BF16, tag="hm_grouped", align_bytes=64)
-            regroup_passes(nc.vector.tensor_copy, hm_grouped[:], hm_rows[:])
-            ha_b = quantise(work_pass, "ha", ha_grouped_b[:].rearrange("p e j -> p (e j)"))
-            hm_before = hm
-            hm = quantise(work_round, "hm", hm_grouped[:].rearrange("p n d j -> p (n d j)"))
-
-            if r == SMALL_LOAD_ROUND + 1:
-                w_grouped = consts.tile([P, H3, PACK], BF16, align_bytes=64)
-                regroup(nc.scalar.copy, w_grouped[:], w_rows[:])
-                bias_ps = psum_ring.tile([P, 4, H3], F32, tag="out_ps")
+            grouped = copies(source.shape[1], passes, rows, bank)
+            if copied is not None:
+                finish(*copied)
+            copied = (source, t, passes, grouped)
+            if i == SMALL_LOAD_CHUNK + 2:
+                w_grouped = consts.tile([P, 1, H3, PACK], BF16, align_bytes=64)
+                regroup(s_copy, w_grouped[:], w_rows[:])
+                bias_ps = psum_ring.tile([P, 4, H3], F32, name="out_ps")
                 nc.tensor.matmul(out=bias_ps[:, 0, :], lhsT=ones[:], rhs=bias_rows[:], start=True, stop=True)
-            if r == SMALL_LOAD_ROUND + 2:
+            if i == SMALL_LOAD_CHUNK + 4:
                 bias_all = consts.tile([P, H3], F32)
-                nc.vector.tensor_copy(out=bias_all[:], in_=bias_ps[:, 0, :])
-                w = quantise(consts, "w", w_grouped[:].rearrange("p h j -> p (h j)"))
+                v_copy(out=bias_all[:], in_=bias_ps[:, 0, :])
+                w = quantise("w", w_grouped[:].rearrange("p n h j -> p (n h j)"), 1)
 
-        t = (ROUNDS - 1) * ROUND_PASSES
-        ha_rows_a = load_events(t)
-        ha_rows_b = load_events(t + 1)
+        last_rows = load(H_A, PASSES - 1, 1)
         event_rows = consts.tile([P, EVENT_TILES, FUSED], BF16)
         nc.sync.dma_start(out=event_rows[:, :, 0:HD], in_=H_mean_M.rearrange("(a p) c -> p a c", p=P))
-
-        multiply(t - 1, ha_b[0], ha_b[1], hm_before[0], hm_before[1])
-        halves = []
-        for h, copy in enumerate((nc.scalar.copy, nc.vector.tensor_copy)):
-            half_grouped = work_pass.tile([P, EVENTS // 2, PACK], BF16, align_bytes=64)
-            regroup(copy, half_grouped[:], ha_rows_a[:, :, h * EVENTS // 2 : (h + 1) * EVENTS // 2])
-            halves.append(half_grouped)
+        finish(*copied)
 
         tile_grouped = consts.tile([P, EVENT_TILES, P, PACK], BF16, align_bytes=64)
         fused_grouped = consts.tile([P, EVENT_TILES, P, PACK], BF16, align_bytes=64)
         result = consts.tile([P, EVENT_TILES, H3], F32)
         words = event_rows[:].rearrange("p a c -> p (a c)").bitcast(F32)
-        event_words = FUSED // 2
-
-        def half_multiply(h):
-            codes, scales = quantise(work_pass, "half", halves[h][:].rearrange("p e j -> p (e j)"))
-            for i in range(EVENT_TILES // 2):
-                nc.tensor.matmul_mx(
-                    out=sums[h * EVENT_TILES // 2 + i][:, 0:HD],
-                    lhsT=codes[:, i * P : (i + 1) * P].bitcast(FP8X4),
-                    lhsT_scale=scales[:, i * P : (i + 1) * P],
-                    rhs=hm[0][:, 0:HD].bitcast(FP8X4),
-                    rhs_scale=hm[1][:, 0:HD],
-                    start=False,
-                    stop=False,
-                )
 
         def tile_copy(copy, a):
-            regroup(copy, tile_grouped[:, a], ha_rows_b[:, :, a * P : (a + 1) * P])
+            regroup(copy, tile_grouped[:, a : a + 1], last_rows[:, :, :, a * P : (a + 1) * P])
 
         def tile_multiply(a):
-            codes, scales = quantise(work_round, "tile", tile_grouped[:, a].rearrange("p e j -> p (e j)"))
-            nc.tensor.matmul_mx(
-                out=sums[a][:, 0:HD],
-                lhsT=codes[:].bitcast(FP8X4),
-                lhsT_scale=scales[:],
-                rhs=hm[0][:, HD : 2 * HD].bitcast(FP8X4),
-                rhs_scale=hm[1][:, HD : 2 * HD],
-                start=False,
-                stop=True,
-            )
+            codes, scales = quantise("tile", tile_grouped[:, a].rearrange("p e j -> p (e j)"), EVENT_TILES)
+            multiply(PASSES - 1, codes[:], scales[:], (a,), True)
 
         def tile_sum(copy, a):
             copy(out=event_rows[:, a, HD:FUSED], in_=sums[a][:, 0:HD])
 
         def tile_transpose(a):
-            word_t = psum_ring.tile([P, 4, P], F32, tag="word_t")
             for u in range(2):
                 nc.tensor.transpose(
-                    word_t[:, u, :], words[:, a * event_words + u : (a + 1) * event_words : 2], identity[:]
+                    sums[a][:, HD + u * P : HD + (u + 1) * P],
+                    words[:, a * EVENT_WORDS + u : (a + 1) * EVENT_WORDS : 2],
+                    identity[:],
                 )
-            return word_t
 
-        def tile_interleave(copy, a, word_t):
+        def tile_interleave(copy, a):
             copy(
                 out=fused_grouped[:, a].rearrange("p e j -> p (e j)").bitcast(F32).rearrange("p (e u) -> p e u", u=2),
-                in_=word_t[:, 0:2, :].rearrange("p u e -> p e u"),
+                in_=sums[a][:, HD : 2 * HD].rearrange("p (u e) -> p e u", u=2),
             )
 
-        def tile_fused(a):
-            return quantise(work_round, "fused", fused_grouped[:, a].rearrange("p e j -> p (e j)"))
-
-        def tile_out(out_ps, slot, codes, scales):
+        def tile_out(a):
+            codes, scales = quantise("fused", fused_grouped[:, a].rearrange("p e j -> p (e j)"), EVENT_TILES)
             nc.tensor.matmul_mx(
-                out=out_ps[:, slot, :],
+                out=out_ps[a // 2][:, a % 2, :],
                 lhsT=codes[:].bitcast(FP8X4),
                 lhsT_scale=scales[:],
                 rhs=w[0][:].bitcast(FP8X4),
@@ -256,57 +224,39 @@ def tile_mymodel_icdm_pa_k_kernel(tc, H_A, H_mean_A, H_mean_M, wEA1, bEA1, out):
                 stop=True,
             )
 
-        def add_bias(a, out_ps, slot, count=1):
+        def pair_store(b):
+            pair = slice(2 * b, 2 * b + 2)
             nc.vector.tensor_tensor(
-                out=result[:, a : a + count, :],
-                in0=out_ps[:, slot : slot + count, :],
-                in1=bias_all[:].unsqueeze(1).to_broadcast([P, count, H3]),
+                out=result[:, pair, :],
+                in0=out_ps[b][:, 0:2, :],
+                in1=bias_all[:].unsqueeze(1).to_broadcast([P, 2, H3]),
                 op=ADD,
             )
-
-        def relu(a, count=1):
-            nc.scalar.activation(out=result[:, a : a + count, :], in_=result[:, a : a + count, :], func=RELU)
-
-        def store(first, last):
+            nc.scalar.activation(out=result[:, pair, :], in_=result[:, pair, :], func=RELU)
             nc.sync.dma_start(
-                out=out[first * P : last * P, :].rearrange("(a p) h -> p a h", p=P), in_=result[:, first:last, :]
+                out=out[2 * b * P : (2 * b + 2) * P, :].rearrange("(a p) h -> p a h", p=P), in_=result[:, pair, :]
             )
 
-        v_copy = nc.vector.tensor_copy
-        s_copy = nc.scalar.copy
-        half_multiply(1)
-        half_multiply(0)
-        tile_copy(s_copy, 2)
-        tile_copy(s_copy, 3)
         tile_copy(v_copy, 0)
-        tile_copy(v_copy, 1)
-        tile_multiply(0)
-        tile_multiply(2)
+        tile_copy(s_copy, 1)
+        tile_copy(v_copy, 2)
+        tile_copy(s_copy, 3)
+        for a in range(EVENT_TILES):
+            tile_multiply(a)
         tile_sum(s_copy, 0)
-        tile_multiply(1)
-        tile_multiply(3)
-        tile_sum(s_copy, 2)
-        wt0 = tile_transpose(0)
-        tile_sum(v_copy, 1)
-        wt2 = tile_transpose(2)
+        tile_sum(s_copy, 1)
+        tile_sum(v_copy, 2)
         tile_sum(v_copy, 3)
-        tile_interleave(s_copy, 0, wt0)
-        wt1 = tile_transpose(1)
-        tile_interleave(s_copy, 2, wt2)
-        wt3 = tile_transpose(3)
-        out_a = psum_ring.tile([P, 4, H3], F32, name="out_a", tag="out_ps")
-        out_b = psum_ring.tile([P, 4, H3], F32, name="out_b", tag="out_ps")
-        tile_out(out_a, 0, *tile_fused(0))
-        tile_interleave(v_copy, 1, wt1)
-        fused2 = tile_fused(2)
-        tile_interleave(s_copy, 3, wt3)
-        tile_out(out_a, 1, *tile_fused(1))
-        tile_out(out_b, 0, *fused2)
-        add_bias(0, out_a, 0, 2)
-        fused3 = tile_fused(3)
-        tile_out(out_b, 1, *fused3)
-        relu(0, 2)
-        store(0, 2)
-        add_bias(2, out_b, 0, 2)
-        relu(2, 2)
-        store(2, 4)
+        for a in range(EVENT_TILES):
+            tile_transpose(a)
+        out_ps = [psum_ring.tile([P, 4, H3], F32, name="out_ps") for b in range(2)]
+        tile_interleave(s_copy, 0)
+        tile_interleave(s_copy, 1)
+        tile_out(0)
+        tile_interleave(v_copy, 2)
+        tile_interleave(s_copy, 3)
+        tile_out(1)
+        tile_out(2)
+        tile_out(3)
+        pair_store(0)
+        pair_store(1)

@@ -24,10 +24,19 @@ PASSES = NODES // K_PASS
 SINGLE_PASSES = 4
 TAIL_PASSES = 4
 
-SCALAR_COLS = {EVENTS: EVENTS // 2, HD: HD // 2}
-
-TENSOR_COLS = 128
-SCALAR_COLS_BESIDE = 296
+TENSOR_COLS = 256
+SHARES = {
+    (HD, 1, False): (("scalar", 0, 1, 0, HD // 2), ("vector", 0, 1, HD // 2, HD)),
+    (HD, 2, False): (("scalar", 0, 1, 0, HD), ("vector", 1, 2, 0, HD)),
+    (HD, 4, False): (
+        ("scalar", 0, 2, 0, HD),
+        ("scalar", 2, 3, 0, HD // 2),
+        ("vector", 2, 3, HD // 2, HD),
+        ("vector", 3, 4, 0, HD),
+    ),
+    (EVENTS, 1, False): (("scalar", 0, 1, 0, EVENTS // 2), ("vector", 0, 1, EVENTS // 2, EVENTS)),
+    (EVENTS, 2, True): (("scalar", 0, 1, TENSOR_COLS, EVENTS), ("vector", 1, 2, 0, EVENTS)),
+}
 
 RUN = 4
 
@@ -89,12 +98,12 @@ def tile_mymodel_icdm_pa_k_kernel(tc, H_A, H_mean_A, H_mean_M, wEA1, bEA1, out):
             return rows[:]
 
         def tensor_regroup(rows):
-            bank = psum_ring.tile([P, 2, TENSOR_COLS, PACK], BF16, name="regrouped")
-            for n in range(2):
+            bank = psum_ring.tile([P, TENSOR_COLS, PACK], BF16, name="regrouped")
+            for j in range(0, PACK, 2):
                 nc.tensor.matmul(
-                    out=bank[:, n].rearrange("p w j -> p j w"),
+                    out=bank[:, :, j : j + 2].rearrange("p w j -> p j w"),
                     lhsT=identity_bf[:],
-                    rhs=rows[:, n, :, 0:TENSOR_COLS],
+                    rhs=rows[:, 0, j : j + 2, 0:TENSOR_COLS],
                     start=True,
                     stop=True,
                 )
@@ -105,14 +114,12 @@ def tile_mymodel_icdm_pa_k_kernel(tc, H_A, H_mean_A, H_mean_M, wEA1, bEA1, out):
             grouped = work.tile(
                 [P, passes, width, PACK], BF16, name=name, tag=name, bufs=GROUPED_BUFS[(width, passes)], align_bytes=64
             )
-            first, last = (0, SCALAR_COLS[width]) if bank is None else (TENSOR_COLS, SCALAR_COLS_BESIDE)
-            regroup(s_copy, grouped[:, :, first:last], rows[:, :, :, first:last])
-            if bank is not None:
-                s_copy(
-                    out=grouped[:, :, 0:TENSOR_COLS].rearrange("p n w j -> p n (w j)"),
-                    in_=bank[:].rearrange("p n w j -> p n (w j)"),
+            for copy, n0, n1, c0, c1 in SHARES[(width, passes, bank is not None)]:
+                regroup(
+                    s_copy if copy == "scalar" else v_copy, grouped[:, n0:n1, c0:c1], rows[:, n0:n1, :, c0:c1]
                 )
-            regroup(v_copy, grouped[:, :, last:width], rows[:, :, :, last:width])
+            if bank is not None:
+                s_copy(out=grouped[:, 0, 0:TENSOR_COLS], in_=bank[:])
             return grouped
 
         def multiply(t, codes, scales, tiles, stop):

@@ -9,7 +9,6 @@ U32 = mybir.dt.uint32
 U8 = mybir.dt.uint8
 FP8X4 = mybir.dt.float8_e4m3fn_x4
 ADD = mybir.AluOpType.add
-RELU = mybir.ActivationFunctionType.Relu
 
 P = 128
 PACK = 4
@@ -134,11 +133,13 @@ def tile_mymodel_icdm_pa_k_kernel(tc, H_A, H_mean_A, H_mean_M, wEA1, bEA1, out):
                     stop=stop,
                 )
 
+        def quantise_chunk(source, passes, grouped):
+            name = "chunk_%d_%d" % (source.shape[1], passes)
+            return quantise(name, grouped[:].rearrange("p n w j -> p (n w j)"), CODES_BUFS)
+
         def finish(source, t, passes, grouped):
             width = source.shape[1]
-            codes, scales = quantise(
-                "chunk_%d_%d" % (width, passes), grouped[:].rearrange("p n w j -> p (n w j)"), CODES_BUFS
-            )
+            codes, scales = quantise_chunk(source, passes, grouped)
             for n in range(passes):
                 cols = slice(n * width, (n + 1) * width)
                 if width == HD:
@@ -151,8 +152,9 @@ def tile_mymodel_icdm_pa_k_kernel(tc, H_A, H_mean_A, H_mean_M, wEA1, bEA1, out):
             chunks += [(H_mean_A, t, 2, False), (H_A, t, 1, False), (H_A, t + 1, 1, False)]
         for t in range(SINGLE_PASSES, PASSES - TAIL_PASSES, 4):
             chunks += [(H_mean_A, t, 4, False), (H_A, t, 2, True), (H_A, t + 2, 2, True)]
-        chunks += [(H_mean_A, PASSES - TAIL_PASSES, TAIL_PASSES, False)]
-        chunks += [(H_A, t, 1, False) for t in range(PASSES - TAIL_PASSES, PASSES - 1)]
+        t = PASSES - TAIL_PASSES
+        chunks += [(H_mean_A, t, 2, False), (H_A, t, 1, False)]
+        chunks += [(H_mean_A, t + 2, 2, False), (H_A, t + 1, 1, False), (H_A, t + 2, 1, False)]
 
         def fetch(i):
             source, t, passes, shared = chunks[i]
@@ -188,7 +190,7 @@ def tile_mymodel_icdm_pa_k_kernel(tc, H_A, H_mean_A, H_mean_M, wEA1, bEA1, out):
         last_rows = load(H_A, PASSES - 1, 1)
         event_rows = consts.tile([P, EVENT_TILES, FUSED], BF16)
         nc.sync.dma_start(out=event_rows[:, :, 0:HD], in_=H_mean_M.rearrange("(a p) c -> p a c", p=P))
-        finish(*copied)
+        codes_before, scales_before = quantise_chunk(H_A, 1, grouped)
 
         tile_grouped = consts.tile([P, EVENT_TILES, P, PACK], BF16, align_bytes=64)
         fused_grouped = consts.tile([P, EVENT_TILES, P, PACK], BF16, align_bytes=64)
@@ -200,6 +202,8 @@ def tile_mymodel_icdm_pa_k_kernel(tc, H_A, H_mean_A, H_mean_M, wEA1, bEA1, out):
 
         def tile_multiply(a):
             codes, scales = quantise("tile", tile_grouped[:, a].rearrange("p e j -> p (e j)"), EVENT_TILES)
+            events = slice(a * P, (a + 1) * P)
+            multiply(PASSES - 2, codes_before[:, events], scales_before[:, events], (a,), False)
             multiply(PASSES - 1, codes[:], scales[:], (a,), True)
 
         def tile_sum(copy, a):
@@ -231,7 +235,7 @@ def tile_mymodel_icdm_pa_k_kernel(tc, H_A, H_mean_A, H_mean_M, wEA1, bEA1, out):
                 stop=True,
             )
 
-        def pair_store(b):
+        def pair_bias(b):
             pair = slice(2 * b, 2 * b + 2)
             nc.vector.tensor_tensor(
                 out=result[:, pair, :],
@@ -239,20 +243,23 @@ def tile_mymodel_icdm_pa_k_kernel(tc, H_A, H_mean_A, H_mean_M, wEA1, bEA1, out):
                 in1=bias_all[:].unsqueeze(1).to_broadcast([P, 2, H3]),
                 op=ADD,
             )
-            nc.scalar.activation(out=result[:, pair, :], in_=result[:, pair, :], func=RELU)
+
+        def pair_store(b):
+            pair = slice(2 * b, 2 * b + 2)
+            nc.vector.tensor_scalar_max(out=result[:, pair, :], in0=result[:, pair, :], scalar1=0.0)
             nc.sync.dma_start(
                 out=out[2 * b * P : (2 * b + 2) * P, :].rearrange("(a p) h -> p a h", p=P), in_=result[:, pair, :]
             )
 
         tile_copy(v_copy, 0)
         tile_copy(s_copy, 1)
-        tile_copy(v_copy, 2)
+        tile_copy(s_copy, 2)
         tile_copy(s_copy, 3)
         for a in range(EVENT_TILES):
             tile_multiply(a)
         tile_sum(s_copy, 0)
-        tile_sum(s_copy, 1)
-        tile_sum(v_copy, 2)
+        tile_sum(v_copy, 1)
+        tile_sum(s_copy, 2)
         tile_sum(v_copy, 3)
         for a in range(EVENT_TILES):
             tile_transpose(a)
@@ -265,5 +272,7 @@ def tile_mymodel_icdm_pa_k_kernel(tc, H_A, H_mean_A, H_mean_M, wEA1, bEA1, out):
         tile_out(1)
         tile_out(2)
         tile_out(3)
+        pair_bias(0)
+        pair_bias(1)
         pair_store(0)
         pair_store(1)

from contextlib import ExitStack

import concourse.mybir as mybir
from concourse.masks import make_identity

BF16 = mybir.dt.bfloat16
F32 = mybir.dt.float32
U32 = mybir.dt.uint32
U8 = mybir.dt.uint8
FP8X4 = mybir.dt.float8_e4m3fn_x4
ADD = mybir.AluOpType.add

P = 128
PACK = 4
K_PASS = P * PACK

NODES, EVENTS, HD, H3 = 16384, 512, 256, 128
FUSED = 2 * HD
EVENT_WORDS = FUSED // 2
EVENT_TILES = EVENTS // P
PASSES = NODES // K_PASS

SINGLE_PASSES = 4
TAIL_PASSES = 4

TENSOR_COLS = 256
SHARES = {
    (HD, 1, False): (("scalar", 0, 1, 0, HD // 2), ("vector", 0, 1, HD // 2, HD)),
    (HD, 2, False): (("scalar", 0, 1, 0, HD), ("vector", 1, 2, 0, HD)),
    (HD, 4, False): (
        ("scalar", 0, 2, 0, HD),
        ("scalar", 2, 3, 0, HD // 2),
        ("vector", 2, 3, HD // 2, HD),
        ("vector", 3, 4, 0, HD),
    ),
    (EVENTS, 1, False): (("scalar", 0, 1, 0, EVENTS // 2), ("vector", 0, 1, EVENTS // 2, EVENTS)),
    (EVENTS, 2, True): (("scalar", 0, 1, TENSOR_COLS, EVENTS), ("vector", 1, 2, 0, EVENTS)),
}

RUN = 4

SMALL_LOAD_CHUNK = 9

ROWS_BUFS = {(HD, 1): 2, (HD, 2): 2, (HD, 4): 3, (EVENTS, 1): 6, (EVENTS, 2): 5}
GROUPED_BUFS = {(HD, 1): 2, (HD, 2): 2, (HD, 4): 2, (EVENTS, 1): 3, (EVENTS, 2): 3}
CODES_BUFS = 3

FLOPS = 2 * NODES * EVENTS * HD + 2 * EVENTS * FUSED * H3


def regroup(copy, grouped, rows):
    copy(
        out=grouped.rearrange("p n (c i) j -> p n c j i", i=RUN),
        in_=rows.rearrange("p n j (c i) -> p n c j i", i=RUN),
    )


def tile_mymodel_icdm_pa_k_kernel(tc, H_A, H_mean_A, H_mean_M, wEA1, bEA1, out):
    nc = tc.nc
    v_copy = nc.vector.tensor_copy
    s_copy = nc.scalar.copy
    with ExitStack() as stack:
        consts = stack.enter_context(tc.tile_pool(name="consts", bufs=1))
        raw = stack.enter_context(tc.tile_pool(name="raw", bufs=2))
        work = stack.enter_context(tc.tile_pool(name="work", bufs=2))
        psum = stack.enter_context(tc.psum_pool(name="psum", bufs=1))
        psum_ring = stack.enter_context(tc.psum_pool(name="psum_ring", bufs=2))
        stack.enter_context(tc.manual_schedule())

        def quantise(name, grouped, bufs):
            words = grouped.shape[1] // PACK
            codes = work.tile([P, words], U32, name=name + "_codes", tag=name + "_codes", bufs=bufs, align_bytes=64)
            scales = work.tile([P, words], U8, name=name + "_scales", tag=name + "_scales", bufs=bufs, align_bytes=64)
            nc.vector.quantize_mx(out=codes[:].bitcast(FP8X4), scales=scales[:], in_=grouped)
            return codes, scales

        identity = consts.tile([P, P], F32)
        make_identity(nc, identity[:])
        identity_bf = consts.tile([P, P], BF16)
        make_identity(nc, identity_bf[:])
        ones = consts.tile([P, P], BF16)
        nc.vector.memset(ones[:], 1.0)
        bias_rows = consts.tile([P, H3], BF16)
        nc.vector.memset(bias_rows[:], 0.0)

        sums = [psum.tile([P, 2 * HD], F32, name="sum%d" % a) for a in range(EVENT_TILES)]
        features = {}

        def load(source, t, passes):
            width = source.shape[1]
            name = "rows_%d_%d" % (width, passes)
            rows = raw.tile([P, passes, PACK, width], BF16, name=name, tag=name, bufs=ROWS_BUFS[(width, passes)])
            nc.sync.dma_start(
                out=rows[:].rearrange("p n j w -> p n (j w)"),
                in_=source[t * K_PASS : (t + passes) * K_PASS, :].rearrange("(n p j) w -> p n (j w)", p=P, j=PACK),
            )
            return rows[:]

        def tensor_regroup(rows):
            bank = psum_ring.tile([P, TENSOR_COLS, PACK], BF16, name="regrouped")
            for j in range(0, PACK, 2):
                nc.tensor.matmul(
                    out=bank[:, :, j : j + 2].rearrange("p w j -> p j w"),
                    lhsT=identity_bf[:],
                    rhs=rows[:, 0, j : j + 2, 0:TENSOR_COLS],
                    start=True,
                    stop=True,
                )
            return bank

        def copies(width, passes, rows, bank):
            name = "grouped_%d_%d" % (width, passes)
            grouped = work.tile(
                [P, passes, width, PACK], BF16, name=name, tag=name, bufs=GROUPED_BUFS[(width, passes)], align_bytes=64
            )
            for copy, n0, n1, c0, c1 in SHARES[(width, passes, bank is not None)]:
                regroup(
                    s_copy if copy == "scalar" else v_copy, grouped[:, n0:n1, c0:c1], rows[:, n0:n1, :, c0:c1]
                )
            if bank is not None:
                s_copy(out=grouped[:, 0, 0:TENSOR_COLS], in_=bank[:])
            return grouped

        def multiply(t, codes, scales, tiles, stop):
            for i, a in enumerate(tiles):
                nc.tensor.matmul_mx(
                    out=sums[a][:, 0:HD],
                    lhsT=codes[:, i * P : (i + 1) * P].bitcast(FP8X4),
                    lhsT_scale=scales[:, i * P : (i + 1) * P],
                    rhs=features[t][0].bitcast(FP8X4),
                    rhs_scale=features[t][1],
                    start=(t == 0),
                    stop=stop,
                )

        def quantise_chunk(source, passes, grouped):
            name = "chunk_%d_%d" % (source.shape[1], passes)
            return quantise(name, grouped[:].rearrange("p n w j -> p (n w j)"), CODES_BUFS)

        def finish(source, t, passes, grouped):
            width = source.shape[1]
            codes, scales = quantise_chunk(source, passes, grouped)
            for n in range(passes):
                cols = slice(n * width, (n + 1) * width)
                if width == HD:
                    features[t + n] = (codes[:, cols], scales[:, cols])
                else:
                    multiply(t + n, codes[:, cols], scales[:, cols], range(EVENT_TILES), False)

        chunks = [(H_mean_A, 0, 1, False), (H_mean_A, 1, 1, False), (H_A, 0, 1, False), (H_A, 1, 1, False)]
        for t in range(2, SINGLE_PASSES, 2):
            chunks += [(H_mean_A, t, 2, False), (H_A, t, 1, False), (H_A, t + 1, 1, False)]
        for t in range(SINGLE_PASSES, PASSES - TAIL_PASSES, 4):
            chunks += [(H_mean_A, t, 4, False), (H_A, t, 2, True), (H_A, t + 2, 2, True)]
        t = PASSES - TAIL_PASSES
        chunks += [(H_mean_A, t, 2, False), (H_A, t, 1, False)]
        chunks += [(H_mean_A, t + 2, 2, False), (H_A, t + 1, 1, False), (H_A, t + 2, 1, False)]

        def fetch(i):
            source, t, passes, shared = chunks[i]
            rows = load(source, t, passes)
            return rows, tensor_regroup(rows) if shared else None

        fetched = fetch(0)
        copied = None
        for i, (source, t, passes, shared) in enumerate(chunks):
            rows, bank = fetched
            if i + 1 < len(chunks):
                fetched = fetch(i + 1)
            if i == SMALL_LOAD_CHUNK:
                w_rows = consts.tile([P, 1, PACK, H3], BF16)
                nc.sync.dma_start(
                    out=w_rows[:].rearrange("p n j h -> p (n j) h"), in_=wEA1.rearrange("(p j) h -> p j h", j=PACK)
                )
                nc.sync.dma_start(out=bias_rows[0:1, :], in_=bEA1.rearrange("(o h) -> o h", o=1))
            grouped = copies(source.shape[1], passes, rows, bank)
            if copied is not None:
                finish(*copied)
            copied = (source, t, passes, grouped)
            if i == SMALL_LOAD_CHUNK + 2:
                w_grouped = consts.tile([P, 1, H3, PACK], BF16, align_bytes=64)
                regroup(s_copy, w_grouped[:], w_rows[:])
                bias_ps = psum_ring.tile([P, 4, H3], F32, name="out_ps")
                nc.tensor.matmul(out=bias_ps[:, 0, :], lhsT=ones[:], rhs=bias_rows[:], start=True, stop=True)
            if i == SMALL_LOAD_CHUNK + 4:
                bias_all = consts.tile([P, H3], F32)
                v_copy(out=bias_all[:], in_=bias_ps[:, 0, :])
                w = quantise("w", w_grouped[:].rearrange("p n h j -> p (n h j)"), 1)

        last_rows = load(H_A, PASSES - 1, 1)
        event_rows = consts.tile([P, EVENT_TILES, FUSED], BF16)
        nc.sync.dma_start(out=event_rows[:, :, 0:HD], in_=H_mean_M.rearrange("(a p) c -> p a c", p=P))
        codes_before, scales_before = quantise_chunk(H_A, 1, grouped)

        tile_grouped = consts.tile([P, EVENT_TILES, P, PACK], BF16, align_bytes=64)
        fused_grouped = consts.tile([P, EVENT_TILES, P, PACK], BF16, align_bytes=64)
        result = consts.tile([P, EVENT_TILES, H3], F32)
        words = event_rows[:].rearrange("p a c -> p (a c)").bitcast(F32)

        def tile_copy(copy, a):
            regroup(copy, tile_grouped[:, a : a + 1], last_rows[:, :, :, a * P : (a + 1) * P])

        def tile_multiply(a):
            codes, scales = quantise("tile", tile_grouped[:, a].rearrange("p e j -> p (e j)"), EVENT_TILES)
            events = slice(a * P, (a + 1) * P)
            multiply(PASSES - 2, codes_before[:, events], scales_before[:, events], (a,), False)
            multiply(PASSES - 1, codes[:], scales[:], (a,), True)

        def tile_sum(copy, a):
            copy(out=event_rows[:, a, HD:FUSED], in_=sums[a][:, 0:HD])

        def tile_transpose(a):
            for u in range(2):
                nc.tensor.transpose(
                    sums[a][:, HD + u * P : HD + (u + 1) * P],
                    words[:, a * EVENT_WORDS + u : (a + 1) * EVENT_WORDS : 2],
                    identity[:],
                )

        def tile_interleave(copy, a):
            copy(
                out=fused_grouped[:, a].rearrange("p e j -> p (e j)").bitcast(F32).rearrange("p (e u) -> p e u", u=2),
                in_=sums[a][:, HD : 2 * HD].rearrange("p (u e) -> p e u", u=2),
            )

        def tile_out(a):
            codes, scales = quantise("fused", fused_grouped[:, a].rearrange("p e j -> p (e j)"), EVENT_TILES)
            nc.tensor.matmul_mx(
                out=out_ps[a // 2][:, a % 2, :],
                lhsT=codes[:].bitcast(FP8X4),
                lhsT_scale=scales[:],
                rhs=w[0][:].bitcast(FP8X4),
                rhs_scale=w[1][:],
                start=True,
                stop=True,
            )

        def pair_bias(b):
            pair = slice(2 * b, 2 * b + 2)
            nc.vector.tensor_tensor(
                out=result[:, pair, :],
                in0=out_ps[b][:, 0:2, :],
                in1=bias_all[:].unsqueeze(1).to_broadcast([P, 2, H3]),
                op=ADD,
            )

        def pair_store(b):
            pair = slice(2 * b, 2 * b + 2)
            nc.vector.tensor_scalar_max(out=result[:, pair, :], in0=result[:, pair, :], scalar1=0.0)
            nc.sync.dma_start(
                out=out[2 * b * P : (2 * b + 2) * P, :].rearrange("(a p) h -> p a h", p=P), in_=result[:, pair, :]
            )

        tile_copy(v_copy, 0)
        tile_copy(s_copy, 1)
        tile_copy(s_copy, 2)
        tile_copy(s_copy, 3)
        for a in range(EVENT_TILES):
            tile_multiply(a)
        tile_sum(s_copy, 0)
        tile_sum(v_copy, 1)
        tile_sum(s_copy, 2)
        tile_sum(v_copy, 3)
        for a in range(EVENT_TILES):
            tile_transpose(a)
        out_ps = [psum_ring.tile([P, 4, H3], F32, name="out_ps") for b in range(2)]
        tile_interleave(s_copy, 0)
        tile_interleave(s_copy, 1)
        tile_out(0)
        tile_interleave(v_copy, 2)
        tile_interleave(s_copy, 3)
        tile_out(1)
        tile_out(2)
        tile_out(3)
        pair_bias(0)
        pair_bias(1)
        pair_store(0)
        pair_store(1)
